import numpy as np
import ml_dtypes


def mxq(x, axis, fmt="e4m3"):
    dtype, down = {"e4m3": (ml_dtypes.float8_e4m3fn, 7), "e5m2": (ml_dtypes.float8_e5m2, 14)}[fmt]
    v = np.moveaxis(np.asarray(x, np.float32).astype(ml_dtypes.bfloat16).astype(np.float64), axis, -1)
    blocks = v.reshape(v.shape[:-1] + (-1, 32))
    amax = np.abs(blocks).max(-1, keepdims=True)
    byte = np.maximum(np.where(amax > 0, np.frexp(amax)[1] - 1 + 127, 0) - down, 1)
    scale = np.exp2(byte - 127.0)
    codes = (blocks / scale).astype(np.float32).astype(dtype).astype(np.float64)
    return np.moveaxis((codes * scale).reshape(v.shape), -1, axis)


WIDE = False


def mx_kscale(k):
    if not WIDE:
        return np.ones(k)
    levels = np.array([10, -10, 5, -5, 0])
    a = np.random.permutation(np.resize(levels, k // 512 * 4)).reshape(k // 512, 4)
    idx = np.arange(k)
    return np.exp2(a[idx // 512, idx % 128 // 32])


BF16 = ml_dtypes.bfloat16


def bf(x):
    return np.asarray(x, np.float32).astype(BF16)


def f64(x):
    return np.asarray(x).astype(np.float64)


E2M1 = np.array([0.0, 0.5, 1.0, 1.5, 2.0, 3.0, 4.0, 6.0, -0.0, -0.5, -1.0, -1.5, -2.0, -3.0, -4.0, -6.0])


def pack_weight(w, fmt):
    k, n = w.shape
    w = f64(bf(w)).reshape(k // 32, 32, n)
    amax = np.abs(w).max(1)
    if fmt == "e4m3":
        byte = np.frexp(amax)[1] - 1 + 127 - 7
    else:
        mant, ex = np.frexp(amax / 6.0)
        byte = np.where(mant > 0.5, ex, ex - 1) + 127
    byte = np.clip(np.where(amax > 0, byte, 1), 1, 254)
    scaled = (w * np.exp2(127.0 - byte)[:, None, :]).reshape(k, n).astype(np.float32)
    by_word = np.ascontiguousarray(scaled.reshape(k // 512, 128, 4, n).transpose(0, 1, 3, 2))
    if fmt == "e4m3":
        words = by_word.astype(ml_dtypes.float8_e4m3fn).view(np.uint8)
    else:
        c = by_word.astype(ml_dtypes.float4_e2m1fn).view(np.uint8) & 0xF
        words = c[..., 0::2] | (c[..., 1::2] << 4)
    return np.ascontiguousarray(words), np.ascontiguousarray(byte.astype(np.uint8).reshape(k // 512, 16, n))


def unpack_weight(words, scales, fmt):
    g, p, n, _ = words.shape
    if fmt == "e4m3":
        vals = np.ascontiguousarray(words).view(ml_dtypes.float8_e4m3fn).astype(np.float64)
    else:
        nib = np.empty((g, p, n, 4), np.uint8)
        nib[..., 0::2] = words & 0xF
        nib[..., 1::2] = words >> 4
        vals = E2M1[nib]
    vals = vals * np.repeat(np.exp2(scales.astype(np.float64) - 127.0), 8, axis=1)[..., None]
    return vals.transpose(0, 1, 3, 2).reshape(g * 512, n)


N, S, K, Yd, Xd = 4096, 4, 16, 512, 256
LOG_2PI = np.log(2.0 * np.pi)
FMT = "e4m3"


def softplus(v):
    return np.maximum(v, 0.0) + np.log(1.0 + np.exp(-np.abs(v)))


def log_softmax(v, axis):
    m = v - v.max(axis, keepdims=True)
    return m - np.log(np.exp(m).sum(axis, keepdims=True))


def mv_gaussian_log_prob(value, mu, sig_diags, event_shape):
    diff = value - mu
    M = np.sum((diff / sig_diags) ** 2, axis=-1)
    half_log_det = np.sum(np.log(sig_diags), axis=-1)
    return -0.5 * (event_shape * LOG_2PI + M) - half_log_det


def setup_inputs():
    s = mx_kscale(Yd)
    Y = bf(np.random.standard_normal((N, Yd)) * 0.5 * s)
    We_mu_words, We_mu_scales = pack_weight(np.random.standard_normal((Yd, Xd)) * 2.0 / np.sqrt(Yd) / s[:, None], FMT)
    be_mu = bf(np.random.standard_normal(Xd) * 0.1)
    We_sig_words, We_sig_scales = pack_weight(np.random.standard_normal((Yd, Xd)) * 1.0 / np.sqrt(Yd) / s[:, None], FMT)
    be_sig = bf(-3.0 + np.random.standard_normal(Xd) * 0.1)
    phi_mus = bf(np.random.standard_normal((K, Xd)) * 3.0 / np.sqrt(Xd))
    phi_sigs = bf(1.0 + (np.random.random_sample((K, Xd)) - 0.5) * 9.0 / np.sqrt(Xd))
    phi_logits = bf(np.random.standard_normal(K))
    return {"Y": Y,
            "We_mu_words": We_mu_words,
            "We_mu_scales": We_mu_scales,
            "be_mu": be_mu,
            "We_sig_words": We_sig_words,
            "We_sig_scales": We_sig_scales,
            "be_sig": be_sig,
            "phi_mus": phi_mus,
            "phi_sigs": phi_sigs,
            "phi_logits": phi_logits}


def reference(Y, We_mu_words, We_mu_scales, be_mu, We_sig_words, We_sig_scales, be_sig, phi_mus, phi_sigs, phi_logits):
    Yq = mxq(f64(Y), 1, "e4m3")
    enc_mu = (Yq @ unpack_weight(We_mu_words, We_mu_scales, FMT)) + f64(be_mu)
    enc_sig = softplus((Yq @ unpack_weight(We_sig_words, We_sig_scales, FMT)) + f64(be_sig)) + 1e-3
    log_pi = log_softmax(f64(phi_logits), -1)
    std_k = enc_sig[:, None, :] + f64(phi_sigs)[None, :, :]
    z_logits = log_pi[None, :] + mv_gaussian_log_prob(enc_mu[:, None, :], f64(phi_mus)[None, :, :], std_k, Xd)
    z_log_probs = log_softmax(z_logits, -1)
    return enc_mu, enc_sig, z_log_probs

@@ -1,0 +1,289 @@
+from contextlib import ExitStack
+
+import concourse.masks as masks
+import concourse.mybir as mybir
+
+F32 = mybir.dt.float32
+BF16 = mybir.dt.bfloat16
+I32 = mybir.dt.int32
+U32 = mybir.dt.uint32
+U8 = mybir.dt.uint8
+FP8X4 = mybir.dt.float8_e4m3fn_x4
+ACT = mybir.ActivationFunctionType
+ALU = mybir.AluOpType
+AXIS = mybir.AxisListType
+
+P = 128
+ROWS = 4096
+YD = 512
+XD = 256
+HALVES = XD // P
+CLUSTERS = 16
+TILES = ROWS // P
+GROUP_TILES = 8
+GROUP_PAIRS = GROUP_TILES // 2
+GROUPS = TILES // GROUP_TILES
+GROUP_ROWS = GROUP_TILES * P
+UNIT_CLUSTERS = 8
+UNITS_PER_GROUP = CLUSTERS // UNIT_CLUSTERS
+MX_COLS = 512
+SIG_FLOOR = 1e-3
+
+ROW_PHI_MU = 0
+ROW_PHI_SIG = CLUSTERS
+ROW_BE_MU = 2 * CLUSTERS
+ROW_BE_SIG = 2 * CLUSTERS + 1
+
+FLOPS = 2 * ROWS * YD * 2 * XD
+
+
+def tile_deepgmm_pa_t_kernel(
+    tc,
+    Y,
+    We_mu_words,
+    We_mu_scales,
+    be_mu,
+    We_sig_words,
+    We_sig_scales,
+    be_sig,
+    phi_mus,
+    phi_sigs,
+    phi_logits,
+    out_0,
+    out_1,
+    out_2,
+):
+    nc = tc.nc
+    y_tiles = Y.rearrange("(p i) k -> p i k", i=TILES)
+    mu_out = out_0.rearrange("(p i) d -> p i d", i=TILES)
+    sig_out = out_1.rearrange("(p i) d -> p i d", i=TILES)
+    z_out = out_2.rearrange("(p i) k -> p i k", i=TILES)
+
+    with ExitStack() as ctx:
+        ctx.enter_context(tc.manual_schedule())
+        const = ctx.enter_context(tc.tile_pool(name="const", bufs=1))
+        keep = ctx.enter_context(tc.tile_pool(name="keep", bufs=1))
+
+        ident = const.tile([P, P], F32)
+        masks.make_identity(nc, ident[:])
+        ones_col = const.tile([P, 1], F32)
+        nc.vector.memset(ones_col[:], 1.0)
+
+        mu_T = keep.tile([P, HALVES, ROWS], F32)
+        sp_T = keep.tile([P, HALVES, ROWS], F32)
+        sum_log = keep.tile([P, TILES, CLUSTERS], F32)
+        stats = keep.tile([P, TILES // 2, CLUSTERS, 6], F32)
+        z = keep.tile([P, TILES, CLUSTERS], F32)
+        z_exp = keep.tile([P, TILES, CLUSTERS], F32)
+        z_max = keep.tile([P, TILES], F32)
+        z_sum = keep.tile([P, TILES], F32)
+        params = const.tile([P, HALVES, P], F32)
+        neg_phi_mu = const.tile([P, HALVES, CLUSTERS], F32)
+        phi_sig_floor = const.tile([P, HALVES, CLUSTERS], F32)
+        logits = const.tile([P, CLUSTERS], F32)
+
+        def rows_to_partitions(bank, source, first_row):
+            for two in range(2):
+                first = first_row + two * P
+                for h in range(HALVES):
+                    nc.tensor.transpose(
+                        out=bank[:, two, h * P : (h + 1) * P], in_=source[:, h, first : first + P], identity=ident[:]
+                    )
+
+        with tc.tile_pool(name="enc", bufs=2) as enc, tc.psum_pool(name="enc_ps", bufs=2) as enc_ps:
+            w_words = enc.tile([P, 2, XD], U32, bufs=1, align_bytes=64)
+            w_planes = enc.tile([P, 2, XD], U8, bufs=1, align_bytes=64)
+            nc.vector.memset(w_planes[:].rearrange("p w n -> p (w n)").bitcast(I32), 0)
+            param_rows_bf = enc.tile([P, XD], BF16, bufs=1)
+            nc.vector.memset(param_rows_bf[:].bitcast(I32), 0)
+            logits_bf = enc.tile([P, CLUSTERS], BF16, bufs=1)
+
+            y_loaded = []
+            for g in range(GROUPS):
+                y_rows = enc.tile([P, GROUP_TILES, YD], BF16, bufs=GROUPS)
+                y_loaded.append(y_rows)
+            nc.sync.dma_start(out=y_loaded[0][:], in_=y_tiles[:, 0:GROUP_TILES, :])
+            for w, (words, scales) in enumerate(((We_mu_words, We_mu_scales), (We_sig_words, We_sig_scales))):
+                nc.sync.dma_start(
+                    out=w_words[:, w, :].bitcast(I32),
+                    in_=words[0].rearrange("p n t -> p (n t)").bitcast(I32),
+                )
+                for quadrant in range(4):
+                    nc.sync.dma_start(
+                        out=w_planes[32 * quadrant : 32 * quadrant + 4, w, :].bitcast(I32),
+                        in_=scales[0, 4 * quadrant : 4 * quadrant + 4, :].bitcast(I32),
+                    )
+            nc.sync.dma_start(out=param_rows_bf[ROW_PHI_MU : ROW_PHI_MU + CLUSTERS, :], in_=phi_mus)
+            nc.sync.dma_start(out=param_rows_bf[ROW_PHI_SIG : ROW_PHI_SIG + CLUSTERS, :], in_=phi_sigs)
+            nc.sync.dma_start(out=param_rows_bf[ROW_BE_MU : ROW_BE_MU + 1, :], in_=be_mu.unsqueeze(0))
+            nc.sync.dma_start(out=param_rows_bf[ROW_BE_SIG : ROW_BE_SIG + 1, :], in_=be_sig.unsqueeze(0))
+            nc.sync.dma_start(out=logits_bf[:], in_=phi_logits.partition_broadcast(P))
+            for g in range(1, GROUPS):
+                nc.sync.dma_start(out=y_loaded[g][:], in_=y_tiles[:, g * GROUP_TILES : (g + 1) * GROUP_TILES, :])
+
+            param_rows = enc.tile([P, XD], F32, bufs=1)
+            nc.vector.tensor_copy(out=param_rows[:], in_=param_rows_bf[:])
+            params_ps = enc_ps.tile([P, HALVES, P], F32, bufs=1)
+            for h in range(HALVES):
+                nc.tensor.transpose(out=params_ps[:, h, :], in_=param_rows[:, h * P : (h + 1) * P], identity=ident[:])
+            nc.vector.tensor_copy(out=params[:], in_=params_ps[:])
+            nc.vector.tensor_scalar(
+                out=neg_phi_mu[:], in0=params[:, :, ROW_PHI_MU : ROW_PHI_MU + CLUSTERS],
+                scalar1=-1.0, scalar2=None, op0=ALU.mult,
+            )
+            nc.vector.tensor_scalar(
+                out=phi_sig_floor[:], in0=params[:, :, ROW_PHI_SIG : ROW_PHI_SIG + CLUSTERS],
+                scalar1=SIG_FLOOR, scalar2=None, op0=ALU.add,
+            )
+            nc.vector.tensor_copy(out=logits[:], in_=logits_bf[:])
+
+            pre_sig = enc.tile([P, HALVES, ROWS], F32, bufs=1)
+            soft = enc.tile([P, HALVES, ROWS], F32, bufs=1)
+
+            for g in range(GROUPS):
+                rows = slice(g * GROUP_ROWS, (g + 1) * GROUP_ROWS)
+                y_words = y_loaded[g][:].rearrange("p j k -> p (j k)").bitcast(F32)
+                grouped = enc.tile([P, GROUP_ROWS * 4], BF16, align_bytes=64)
+                grouped_words = grouped[:].bitcast(F32).rearrange("p (n u) -> p n u", u=2)
+                for pair in range(GROUP_PAIRS):
+                    y_T = enc_ps.tile([P, 2, 2 * P], F32, tag="turned")
+                    for two in range(2):
+                        first_word = (2 * pair + two) * (YD // 2)
+                        for u in range(2):
+                            nc.tensor.transpose(
+                                out=y_T[:, u, two * P : (two + 1) * P],
+                                in_=y_words[:, first_word + u : first_word + YD // 2 : 2],
+                                identity=ident[:],
+                            )
+                    nc.vector.tensor_copy(
+                        out=grouped_words[:, 2 * pair * P : (2 * pair + 2) * P, :],
+                        in_=y_T[:].rearrange("p u n -> p n u"),
+                    )
+                y_codes = enc.tile([P, GROUP_ROWS], U32, align_bytes=64)
+                y_scales = enc.tile([P, GROUP_ROWS], U8, align_bytes=64)
+                nc.vector.quantize_mx(out=y_codes[:].bitcast(FP8X4), scales=y_scales[:], in_=grouped[:])
+
+                for w, (target, bias_row) in enumerate(((mu_T, ROW_BE_MU), (pre_sig, ROW_BE_SIG))):
+                    for h in range(HALVES):
+                        for c in range(GROUP_ROWS // MX_COLS):
+                            cols = slice(c * MX_COLS, (c + 1) * MX_COLS)
+                            dest = slice(g * GROUP_ROWS + c * MX_COLS, g * GROUP_ROWS + (c + 1) * MX_COLS)
+                            acc = enc_ps.tile([P, MX_COLS], F32, bufs=3)
+                            nc.tensor.matmul_mx(
+                                out=acc[:],
+                                lhsT=w_words[:, w, h * P : (h + 1) * P].bitcast(FP8X4),
+                                lhsT_scale=w_planes[:, w, h * P : (h + 1) * P],
+                                rhs=y_codes[:, cols].bitcast(FP8X4),
+                                rhs_scale=y_scales[:, cols],
+                                start=True,
+                                stop=True,
+                            )
+                            nc.vector.tensor_scalar(
+                                out=target[:, h, dest], in0=acc[:],
+                                scalar1=params[:, h, bias_row : bias_row + 1], scalar2=None, op0=ALU.add,
+                            )
+                nc.vector.scalar_tensor_tensor(
+                    out=soft[:, :, rows], in0=pre_sig[:, :, rows], scalar=-1.0, in1=pre_sig[:, :, rows],
+                    op0=ALU.mult, op1=ALU.min,
+                )
+            for g in range(GROUPS):
+                rows = slice(g * GROUP_ROWS, (g + 1) * GROUP_ROWS)
+                nc.scalar.activation(out=soft[:, :, rows], in_=soft[:, :, rows], func=ACT.Exp)
+            for g in range(GROUPS):
+                rows = slice(g * GROUP_ROWS, (g + 1) * GROUP_ROWS)
+                nc.scalar.activation(out=soft[:, :, rows], in_=soft[:, :, rows], func=ACT.Ln, bias=ones_col[:])
+                nc.vector.scalar_tensor_tensor(
+                    out=sp_T[:, :, rows], in0=pre_sig[:, :, rows], scalar=0.0, in1=soft[:, :, rows],
+                    op0=ALU.max, op1=ALU.add,
+                )
+            for g in range(GROUPS):
+                for source, floor, dram in ((mu_T, 0.0, mu_out), (sp_T, SIG_FLOOR, sig_out)):
+                    out_rows = enc.tile([P, GROUP_TILES, XD], F32)
+                    for pair in range(GROUP_PAIRS):
+                        turned = enc_ps.tile([P, 2, XD], F32, tag="turned")
+                        rows_to_partitions(turned, source, (g * GROUP_TILES + 2 * pair) * P)
+                        nc.vector.tensor_scalar(
+                            out=out_rows[:, 2 * pair : 2 * pair + 2, :], in0=turned[:],
+                            scalar1=floor, scalar2=None, op0=ALU.add,
+                        )
+                    nc.sync.dma_start(out=dram[:, g * GROUP_TILES : (g + 1) * GROUP_TILES, :], in_=out_rows[:])
+
+        transit = ctx.enter_context(tc.tile_pool(name="transit", bufs=2))
+        slices = ctx.enter_context(tc.tile_pool(name="slices", bufs=UNIT_CLUSTERS + 2))
+        banks = ctx.enter_context(tc.psum_pool(name="banks", bufs=3))
+
+        def add_per_dimension(out_tile, source, column, g, k):
+            rows = slice(g * GROUP_ROWS, (g + 1) * GROUP_ROWS)
+            for h in range(HALVES):
+                nc.gpsimd.tensor_scalar(
+                    out=out_tile[:, h, :], in0=source[:, h, rows],
+                    scalar1=column[:, h, k : k + 1], scalar2=1.0, op0=ALU.add, op1=ALU.mult,
+                )
+
+        def sum_of_squares(work, g, k):
+            for pair in range(GROUP_PAIRS):
+                nc.vector.bn_stats(
+                    out=stats[:, g * GROUP_PAIRS + pair, k, :],
+                    in_=work[:, 2 * pair : 2 * pair + 2, :].rearrange("p j d -> p d j"),
+                )
+
+        unsummed = []
+        for g in range(GROUPS):
+            for unit in range(UNITS_PER_GROUP):
+                works = []
+                for kq in range(UNIT_CLUSTERS):
+                    k = unit * UNIT_CLUSTERS + kq
+                    std_T = transit.tile([P, HALVES, GROUP_ROWS], F32)
+                    add_per_dimension(std_T, sp_T, phi_sig_floor, g, k)
+                    work = slices.tile([P, GROUP_TILES, XD], F32)
+                    works.append((work, g, k))
+                    for pair in range(GROUP_PAIRS):
+                        std = banks.tile([P, 2, XD], F32)
+                        rows_to_partitions(std, std_T, 2 * pair * P)
+                        for two in range(2):
+                            j = 2 * pair + two
+                            nc.scalar.activation(
+                                out=work[:, j, :], in_=std[:, two, :], func=ACT.Ln,
+                                accum_out=sum_log[:, g * GROUP_TILES + j, k : k + 1],
+                            )
+                    if unsummed:
+                        sum_of_squares(*unsummed[kq])
+                for work, g, k in works:
+                    diff_T = transit.tile([P, HALVES, GROUP_ROWS], F32)
+                    add_per_dimension(diff_T, mu_T, neg_phi_mu, g, k)
+                    nc.scalar.activation(out=work[:], in_=work[:], func=ACT.Exp, scale=-1.0)
+                    for pair in range(GROUP_PAIRS):
+                        diff = banks.tile([P, 2, XD], F32)
+                        rows_to_partitions(diff, diff_T, 2 * pair * P)
+                        nc.vector.tensor_tensor(
+                            out=work[:, 2 * pair : 2 * pair + 2, :], in0=diff[:],
+                            in1=work[:, 2 * pair : 2 * pair + 2, :], op=ALU.mult,
+                        )
+                unsummed = works
+        for item in unsummed:
+            sum_of_squares(*item)
+
+        by_tile = stats[:].rearrange("p a k (j c) -> p a j k c", c=3)
+        mean = by_tile[:, :, :, :, 1]
+        spread = by_tile[:, :, :, :, 2]
+        z_pairs = z[:].rearrange("p (a j) k -> p a j k", j=2)
+        nc.vector.tensor_tensor(out=z_pairs, in0=mean, in1=mean, op=ALU.mult)
+        nc.vector.tensor_scalar(out=z[:], in0=z[:], scalar1=float(XD), scalar2=None, op0=ALU.mult)
+        nc.vector.tensor_tensor(out=z_pairs, in0=z_pairs, in1=spread, op=ALU.add)
+        nc.vector.scalar_tensor_tensor(
+            out=z[:], in0=z[:], scalar=-0.5, in1=sum_log[:], op0=ALU.mult, op1=ALU.subtract
+        )
+        nc.vector.tensor_tensor(
+            out=z[:], in0=z[:], in1=logits[:].unsqueeze(1).to_broadcast([P, TILES, CLUSTERS]), op=ALU.add
+        )
+        nc.vector.tensor_reduce(out=z_max[:], in_=z[:], axis=AXIS.X, op=ALU.max)
+        nc.vector.tensor_tensor(
+            out=z[:], in0=z[:], in1=z_max[:].unsqueeze(2).to_broadcast([P, TILES, CLUSTERS]), op=ALU.subtract
+        )
+        nc.scalar.activation(out=z_exp[:], in_=z[:], func=ACT.Exp)
+        nc.vector.tensor_reduce(out=z_sum[:], in_=z_exp[:], axis=AXIS.X, op=ALU.add)
+        nc.scalar.activation(out=z_sum[:], in_=z_sum[:], func=ACT.Ln)
+        nc.vector.tensor_tensor(
+            out=z[:], in0=z[:], in1=z_sum[:].unsqueeze(2).to_broadcast([P, TILES, CLUSTERS]), op=ALU.subtract
+        )
+        nc.sync.dma_start(out=z_out, in_=z[:])

@@ -27,6 +27,11 @@ GROUP_ROWS = GROUP_TILES * P
 UNIT_CLUSTERS = 8
 UNITS_PER_GROUP = CLUSTERS // UNIT_CLUSTERS
 MX_COLS = 512
+STEPS_PER_GROUP = 2 * CLUSTERS
+ENCODER_STAGES = GROUP_PAIRS + 1 + 2 * HALVES * (GROUP_ROWS // MX_COLS) + 5
+TRANSIT_BUFS = 3
+assert UNIT_CLUSTERS <= ENCODER_STAGES - 4 < 2 * UNIT_CLUSTERS
+assert 2 * UNIT_CLUSTERS <= ENCODER_STAGES - 2 < 3 * UNIT_CLUSTERS
 SIG_FLOOR = 1e-3
 
 ROW_PHI_MU = 0
@@ -62,162 +67,213 @@ def tile_deepgmm_pa_t_kernel(
     with ExitStack() as ctx:
         ctx.enter_context(tc.manual_schedule())
         const = ctx.enter_context(tc.tile_pool(name="const", bufs=1))
-        keep = ctx.enter_context(tc.tile_pool(name="keep", bufs=1))
+        enc = ctx.enter_context(tc.tile_pool(name="enc", bufs=1))
+        latent = ctx.enter_context(tc.tile_pool(name="latent", bufs=2))
+        transit = ctx.enter_context(tc.tile_pool(name="transit", bufs=TRANSIT_BUFS))
+        slices = ctx.enter_context(tc.tile_pool(name="slices", bufs=UNIT_CLUSTERS + 2))
+        banks = ctx.enter_context(tc.psum_pool(name="banks", bufs=3))
 
         ident = const.tile([P, P], F32)
         masks.make_identity(nc, ident[:])
         ones_col = const.tile([P, 1], F32)
         nc.vector.memset(ones_col[:], 1.0)
+        w_words = const.tile([P, 2, XD], U32, align_bytes=64)
+        w_planes = const.tile([P, 2, XD], U8, align_bytes=64)
+        nc.vector.memset(w_planes[:].rearrange("p w n -> p (w n)").bitcast(I32), 0)
+        param_rows_bf = const.tile([P, XD], BF16)
+        nc.vector.memset(param_rows_bf[:].bitcast(I32), 0)
+        logits_bf = const.tile([P, CLUSTERS], BF16)
 
-        mu_T = keep.tile([P, HALVES, ROWS], F32)
-        sp_T = keep.tile([P, HALVES, ROWS], F32)
-        sum_log = keep.tile([P, TILES, CLUSTERS], F32)
-        stats = keep.tile([P, TILES // 2, CLUSTERS, 6], F32)
-        z = keep.tile([P, TILES, CLUSTERS], F32)
-        z_exp = keep.tile([P, TILES, CLUSTERS], F32)
-        z_max = keep.tile([P, TILES], F32)
-        z_sum = keep.tile([P, TILES], F32)
+        def load_y(g):
+            y_rows = enc.tile([P, GROUP_TILES, YD], BF16, name="y_rows")
+            nc.sync.dma_start(out=y_rows[:], in_=y_tiles[:, g * GROUP_TILES : (g + 1) * GROUP_TILES, :])
+            return y_rows
+
+        y_loaded = {0: load_y(0)}
+        nc.sync.dma_start(out=param_rows_bf[ROW_PHI_MU : ROW_PHI_MU + CLUSTERS, :], in_=phi_mus)
+        nc.sync.dma_start(out=param_rows_bf[ROW_PHI_SIG : ROW_PHI_SIG + CLUSTERS, :], in_=phi_sigs)
+        nc.sync.dma_start(out=param_rows_bf[ROW_BE_MU : ROW_BE_MU + 1, :], in_=be_mu.unsqueeze(0))
+        nc.sync.dma_start(out=param_rows_bf[ROW_BE_SIG : ROW_BE_SIG + 1, :], in_=be_sig.unsqueeze(0))
+        for w, (words, scales) in enumerate(((We_mu_words, We_mu_scales), (We_sig_words, We_sig_scales))):
+            nc.sync.dma_start(
+                out=w_words[:, w, :].bitcast(I32),
+                in_=words[0].rearrange("p n t -> p (n t)").bitcast(I32),
+            )
+            for quadrant in range(4):
+                nc.sync.dma_start(
+                    out=w_planes[32 * quadrant : 32 * quadrant + 4, w, :].bitcast(I32),
+                    in_=scales[0, 4 * quadrant : 4 * quadrant + 4, :].bitcast(I32),
+                )
+        nc.sync.dma_start(out=logits_bf[:], in_=phi_logits.partition_broadcast(P))
+
+        param_rows = const.tile([P, XD], F32)
+        nc.vector.tensor_copy(out=param_rows[:], in_=param_rows_bf[:])
+        params_ps = banks.tile([P, HALVES, P], F32, tag="aux", bufs=2)
+        for h in range(HALVES):
+            nc.tensor.transpose(out=params_ps[:, h, :], in_=param_rows[:, h * P : (h + 1) * P], identity=ident[:])
         params = const.tile([P, HALVES, P], F32)
+        nc.vector.tensor_copy(out=params[:], in_=params_ps[:])
         neg_phi_mu = const.tile([P, HALVES, CLUSTERS], F32)
+        nc.vector.tensor_scalar(
+            out=neg_phi_mu[:], in0=params[:, :, ROW_PHI_MU : ROW_PHI_MU + CLUSTERS],
+            scalar1=-1.0, scalar2=None, op0=ALU.mult,
+        )
         phi_sig_floor = const.tile([P, HALVES, CLUSTERS], F32)
+        nc.vector.tensor_scalar(
+            out=phi_sig_floor[:], in0=params[:, :, ROW_PHI_SIG : ROW_PHI_SIG + CLUSTERS],
+            scalar1=SIG_FLOOR, scalar2=None, op0=ALU.add,
+        )
         logits = const.tile([P, CLUSTERS], F32)
+        nc.vector.tensor_copy(out=logits[:], in_=logits_bf[:])
 
-        def rows_to_partitions(bank, source, first_row):
+        sum_log = const.tile([P, TILES, CLUSTERS], F32)
+        stats = const.tile([P, TILES // 2, CLUSTERS, 6], F32)
+
+        def rows_to_partitions(bank, source, pair):
             for two in range(2):
-                first = first_row + two * P
+                first = (2 * pair + two) * P
                 for h in range(HALVES):
                     nc.tensor.transpose(
                         out=bank[:, two, h * P : (h + 1) * P], in_=source[:, h, first : first + P], identity=ident[:]
                     )
 
-        with tc.tile_pool(name="enc", bufs=2) as enc, tc.psum_pool(name="enc_ps", bufs=2) as enc_ps:
-            w_words = enc.tile([P, 2, XD], U32, bufs=1, align_bytes=64)
-            w_planes = enc.tile([P, 2, XD], U8, bufs=1, align_bytes=64)
-            nc.vector.memset(w_planes[:].rearrange("p w n -> p (w n)").bitcast(I32), 0)
-            param_rows_bf = enc.tile([P, XD], BF16, bufs=1)
-            nc.vector.memset(param_rows_bf[:].bitcast(I32), 0)
-            logits_bf = enc.tile([P, CLUSTERS], BF16, bufs=1)
+        mu_T = {}
+        sp_T = {}
 
-            y_loaded = []
-            for g in range(GROUPS):
-                y_rows = enc.tile([P, GROUP_TILES, YD], BF16, bufs=GROUPS)
-                y_loaded.append(y_rows)
-            nc.sync.dma_start(out=y_loaded[0][:], in_=y_tiles[:, 0:GROUP_TILES, :])
-            for w, (words, scales) in enumerate(((We_mu_words, We_mu_scales), (We_sig_words, We_sig_scales))):
-                nc.sync.dma_start(
-                    out=w_words[:, w, :].bitcast(I32),
-                    in_=words[0].rearrange("p n t -> p (n t)").bitcast(I32),
-                )
-                for quadrant in range(4):
-                    nc.sync.dma_start(
-                        out=w_planes[32 * quadrant : 32 * quadrant + 4, w, :].bitcast(I32),
-                        in_=scales[0, 4 * quadrant : 4 * quadrant + 4, :].bitcast(I32),
-                    )
-            nc.sync.dma_start(out=param_rows_bf[ROW_PHI_MU : ROW_PHI_MU + CLUSTERS, :], in_=phi_mus)
-            nc.sync.dma_start(out=param_rows_bf[ROW_PHI_SIG : ROW_PHI_SIG + CLUSTERS, :], in_=phi_sigs)
-            nc.sync.dma_start(out=param_rows_bf[ROW_BE_MU : ROW_BE_MU + 1, :], in_=be_mu.unsqueeze(0))
-            nc.sync.dma_start(out=param_rows_bf[ROW_BE_SIG : ROW_BE_SIG + 1, :], in_=be_sig.unsqueeze(0))
-            nc.sync.dma_start(out=logits_bf[:], in_=phi_logits.partition_broadcast(P))
-            for g in range(1, GROUPS):
-                nc.sync.dma_start(out=y_loaded[g][:], in_=y_tiles[:, g * GROUP_TILES : (g + 1) * GROUP_TILES, :])
+        def encoder_stages(g):
+            tiles = {}
 
-            param_rows = enc.tile([P, XD], F32, bufs=1)
-            nc.vector.tensor_copy(out=param_rows[:], in_=param_rows_bf[:])
-            params_ps = enc_ps.tile([P, HALVES, P], F32, bufs=1)
-            for h in range(HALVES):
-                nc.tensor.transpose(out=params_ps[:, h, :], in_=param_rows[:, h * P : (h + 1) * P], identity=ident[:])
-            nc.vector.tensor_copy(out=params[:], in_=params_ps[:])
-            nc.vector.tensor_scalar(
-                out=neg_phi_mu[:], in0=params[:, :, ROW_PHI_MU : ROW_PHI_MU + CLUSTERS],
-                scalar1=-1.0, scalar2=None, op0=ALU.mult,
-            )
-            nc.vector.tensor_scalar(
-                out=phi_sig_floor[:], in0=params[:, :, ROW_PHI_SIG : ROW_PHI_SIG + CLUSTERS],
-                scalar1=SIG_FLOOR, scalar2=None, op0=ALU.add,
-            )
-            nc.vector.tensor_copy(out=logits[:], in_=logits_bf[:])
-
-            pre_sig = enc.tile([P, HALVES, ROWS], F32, bufs=1)
-            soft = enc.tile([P, HALVES, ROWS], F32, bufs=1)
-
-            for g in range(GROUPS):
-                rows = slice(g * GROUP_ROWS, (g + 1) * GROUP_ROWS)
+            def turn_y(pair):
+                if pair == 0:
+                    tiles["grouped"] = enc.tile([P, GROUP_ROWS * 4], BF16, name="grouped", align_bytes=64)
                 y_words = y_loaded[g][:].rearrange("p j k -> p (j k)").bitcast(F32)
-                grouped = enc.tile([P, GROUP_ROWS * 4], BF16, align_bytes=64)
-                grouped_words = grouped[:].bitcast(F32).rearrange("p (n u) -> p n u", u=2)
-                for pair in range(GROUP_PAIRS):
-                    y_T = enc_ps.tile([P, 2, 2 * P], F32, tag="turned")
-                    for two in range(2):
-                        first_word = (2 * pair + two) * (YD // 2)
-                        for u in range(2):
-                            nc.tensor.transpose(
-                                out=y_T[:, u, two * P : (two + 1) * P],
-                                in_=y_words[:, first_word + u : first_word + YD // 2 : 2],
-                                identity=ident[:],
-                            )
-                    nc.vector.tensor_copy(
-                        out=grouped_words[:, 2 * pair * P : (2 * pair + 2) * P, :],
-                        in_=y_T[:].rearrange("p u n -> p n u"),
-                    )
-                y_codes = enc.tile([P, GROUP_ROWS], U32, align_bytes=64)
-                y_scales = enc.tile([P, GROUP_ROWS], U8, align_bytes=64)
-                nc.vector.quantize_mx(out=y_codes[:].bitcast(FP8X4), scales=y_scales[:], in_=grouped[:])
+                grouped_words = tiles["grouped"][:].bitcast(F32).rearrange("p (n u) -> p n u", u=2)
+                y_T = banks.tile([P, 2, 2 * P], F32, tag="aux", bufs=2)
+                for two in range(2):
+                    first_word = (2 * pair + two) * (YD // 2)
+                    for u in range(2):
+                        nc.tensor.transpose(
+                            out=y_T[:, u, two * P : (two + 1) * P],
+                            in_=y_words[:, first_word + u : first_word + YD // 2 : 2],
+                            identity=ident[:],
+                        )
+                nc.vector.tensor_copy(
+                    out=grouped_words[:, 2 * pair * P : (2 * pair + 2) * P, :],
+                    in_=y_T[:].rearrange("p u n -> p n u"),
+                )
 
-                for w, (target, bias_row) in enumerate(((mu_T, ROW_BE_MU), (pre_sig, ROW_BE_SIG))):
-                    for h in range(HALVES):
-                        for c in range(GROUP_ROWS // MX_COLS):
-                            cols = slice(c * MX_COLS, (c + 1) * MX_COLS)
-                            dest = slice(g * GROUP_ROWS + c * MX_COLS, g * GROUP_ROWS + (c + 1) * MX_COLS)
-                            acc = enc_ps.tile([P, MX_COLS], F32, bufs=3)
-                            nc.tensor.matmul_mx(
-                                out=acc[:],
-                                lhsT=w_words[:, w, h * P : (h + 1) * P].bitcast(FP8X4),
-                                lhsT_scale=w_planes[:, w, h * P : (h + 1) * P],
-                                rhs=y_codes[:, cols].bitcast(FP8X4),
-                                rhs_scale=y_scales[:, cols],
-                                start=True,
-                                stop=True,
-                            )
-                            nc.vector.tensor_scalar(
-                                out=target[:, h, dest], in0=acc[:],
-                                scalar1=params[:, h, bias_row : bias_row + 1], scalar2=None, op0=ALU.add,
-                            )
+            def quantise():
+                if g + 1 < GROUPS:
+                    y_loaded[g + 1] = load_y(g + 1)
+                tiles["codes"] = enc.tile([P, GROUP_ROWS], U32, name="y_codes", align_bytes=64)
+                tiles["scales"] = enc.tile([P, GROUP_ROWS], U8, name="y_scales", align_bytes=64)
+                nc.vector.quantize_mx(
+                    out=tiles["codes"][:].bitcast(FP8X4), scales=tiles["scales"][:], in_=tiles["grouped"][:]
+                )
+                tiles["pre_sig"] = enc.tile([P, HALVES, GROUP_ROWS], F32, name="pre_sig")
+                mu_T[g] = latent.tile([P, HALVES, GROUP_ROWS], F32, name="mu_T")
+
+            def product(w, h, c):
+                cols = slice(c * MX_COLS, (c + 1) * MX_COLS)
+                acc = banks.tile([P, MX_COLS], F32, tag="aux", bufs=2)
+                nc.tensor.matmul_mx(
+                    out=acc[:],
+                    lhsT=w_words[:, w, h * P : (h + 1) * P].bitcast(FP8X4),
+                    lhsT_scale=w_planes[:, w, h * P : (h + 1) * P],
+                    rhs=tiles["codes"][:, cols].bitcast(FP8X4),
+                    rhs_scale=tiles["scales"][:, cols],
+                    start=True,
+                    stop=True,
+                )
+                target, bias_row = ((mu_T[g], ROW_BE_MU), (tiles["pre_sig"], ROW_BE_SIG))[w]
+                nc.vector.tensor_scalar(
+                    out=target[:, h, cols], in0=acc[:],
+                    scalar1=params[:, h, bias_row : bias_row + 1], scalar2=None, op0=ALU.add,
+                )
+
+            def minus_abs():
+                tiles["soft"] = enc.tile([P, HALVES, GROUP_ROWS], F32, name="soft")
                 nc.vector.scalar_tensor_tensor(
-                    out=soft[:, :, rows], in0=pre_sig[:, :, rows], scalar=-1.0, in1=pre_sig[:, :, rows],
+                    out=tiles["soft"][:], in0=tiles["pre_sig"][:], scalar=-1.0, in1=tiles["pre_sig"][:],
                     op0=ALU.mult, op1=ALU.min,
                 )
-            for g in range(GROUPS):
-                rows = slice(g * GROUP_ROWS, (g + 1) * GROUP_ROWS)
-                nc.scalar.activation(out=soft[:, :, rows], in_=soft[:, :, rows], func=ACT.Exp)
-            for g in range(GROUPS):
-                rows = slice(g * GROUP_ROWS, (g + 1) * GROUP_ROWS)
-                nc.scalar.activation(out=soft[:, :, rows], in_=soft[:, :, rows], func=ACT.Ln, bias=ones_col[:])
+
+            def soft_exp():
+                nc.scalar.activation(out=tiles["soft"][:], in_=tiles["soft"][:], func=ACT.Exp)
+
+            def soft_log():
+                nc.scalar.activation(out=tiles["soft"][:], in_=tiles["soft"][:], func=ACT.Ln, bias=ones_col[:])
+
+            def softplus():
+                sp_T[g] = latent.tile([P, HALVES, GROUP_ROWS], F32, name="sp_T")
                 nc.vector.scalar_tensor_tensor(
-                    out=sp_T[:, :, rows], in0=pre_sig[:, :, rows], scalar=0.0, in1=soft[:, :, rows],
+                    out=sp_T[g][:], in0=tiles["pre_sig"][:], scalar=0.0, in1=tiles["soft"][:],
                     op0=ALU.max, op1=ALU.add,
                 )
-            for g in range(GROUPS):
-                for source, floor, dram in ((mu_T, 0.0, mu_out), (sp_T, SIG_FLOOR, sig_out)):
-                    out_rows = enc.tile([P, GROUP_TILES, XD], F32)
-                    for pair in range(GROUP_PAIRS):
-                        turned = enc_ps.tile([P, 2, XD], F32, tag="turned")
-                        rows_to_partitions(turned, source, (g * GROUP_TILES + 2 * pair) * P)
-                        nc.vector.tensor_scalar(
-                            out=out_rows[:, 2 * pair : 2 * pair + 2, :], in0=turned[:],
-                            scalar1=floor, scalar2=None, op0=ALU.add,
-                        )
-                    nc.sync.dma_start(out=dram[:, g * GROUP_TILES : (g + 1) * GROUP_TILES, :], in_=out_rows[:])
 
-        transit = ctx.enter_context(tc.tile_pool(name="transit", bufs=2))
-        slices = ctx.enter_context(tc.tile_pool(name="slices", bufs=UNIT_CLUSTERS + 2))
-        banks = ctx.enter_context(tc.psum_pool(name="banks", bufs=3))
+            stages = [lambda pair=pair: turn_y(pair) for pair in range(GROUP_PAIRS)]
+            stages.append(quantise)
+            for w in (1, 0):
+                stages.extend(
+                    lambda w=w, h=h, c=c: product(w, h, c)
+                    for h in range(HALVES)
+                    for c in range(GROUP_ROWS // MX_COLS)
+                )
+                if w == 1:
+                    stages.append(minus_abs)
+            stages.append(None)
+            stages.append(soft_exp)
+            stages.append(soft_log)
+            stages.append(softplus)
+            return stages
 
-        def add_per_dimension(out_tile, source, column, g, k):
-            rows = slice(g * GROUP_ROWS, (g + 1) * GROUP_ROWS)
+        def output_stages(g):
+            def emit(source, floor, dram, pair):
+                turned = banks.tile([P, 2, XD], F32, tag="aux", bufs=2)
+                rows_to_partitions(turned, source, pair)
+                out_rows = enc.tile([P, 2, XD], F32, name="out_rows", bufs=3)
+                nc.vector.tensor_scalar(out=out_rows[:], in0=turned[:], scalar1=floor, scalar2=None, op0=ALU.add)
+                first_tile = g * GROUP_TILES + 2 * pair
+                nc.sync.dma_start(out=dram[:, first_tile : first_tile + 2, :], in_=out_rows[:])
+
+            return [
+                lambda source=source, floor=floor, dram=dram, pair=pair: emit(source, floor, dram, pair)
+                for source, floor, dram in ((mu_T[g], 0.0, mu_out), (sp_T[g], SIG_FLOOR, sig_out))
+                for pair in range(GROUP_PAIRS)
+            ]
+
+        def add_per_dimension(out_tile, source, column, k):
             for h in range(HALVES):
                 nc.gpsimd.tensor_scalar(
-                    out=out_tile[:, h, :], in0=source[:, h, rows],
+                    out=out_tile[:, h, :], in0=source[:, h, :],
                     scalar1=column[:, h, k : k + 1], scalar2=1.0, op0=ALU.add, op1=ALU.mult,
+                )
+
+        def log_of_std(g, k):
+            std_T = transit.tile([P, HALVES, GROUP_ROWS], F32, name="std_T")
+            add_per_dimension(std_T, sp_T[g], phi_sig_floor, k)
+            work = slices.tile([P, GROUP_TILES, XD], F32, name="work")
+            for pair in range(GROUP_PAIRS):
+                std = banks.tile([P, 2, XD], F32, name="std")
+                rows_to_partitions(std, std_T, pair)
+                for two in range(2):
+                    j = 2 * pair + two
+                    nc.scalar.activation(
+                        out=work[:, j, :], in_=std[:, two, :], func=ACT.Ln,
+                        accum_out=sum_log[:, g * GROUP_TILES + j, k : k + 1],
+                    )
+            return work
+
+        def scaled_difference(work, g, k):
+            diff_T = transit.tile([P, HALVES, GROUP_ROWS], F32, name="diff_T")
+            add_per_dimension(diff_T, mu_T[g], neg_phi_mu, k)
+            nc.scalar.activation(out=work[:], in_=work[:], func=ACT.Exp, scale=-1.0)
+            for pair in range(GROUP_PAIRS):
+                diff = banks.tile([P, 2, XD], F32, name="diff")
+                rows_to_partitions(diff, diff_T, pair)
+                nc.vector.tensor_tensor(
+                    out=work[:, 2 * pair : 2 * pair + 2, :], in0=diff[:],
+                    in1=work[:, 2 * pair : 2 * pair + 2, :], op=ALU.mult,
                 )
 
         def sum_of_squares(work, g, k):
@@ -227,38 +283,31 @@ def tile_deepgmm_pa_t_kernel(
                     in_=work[:, 2 * pair : 2 * pair + 2, :].rearrange("p j d -> p d j"),
                 )
 
+        for stage in encoder_stages(0):
+            if stage is not None:
+                stage()
+
         unsummed = []
         for g in range(GROUPS):
+            side_work = encoder_stages(g + 1) if g + 1 < GROUPS else [None] * ENCODER_STAGES
+            assert len(side_work) == ENCODER_STAGES
+            side_work = side_work + output_stages(g) + [None] * (STEPS_PER_GROUP - ENCODER_STAGES - 2 * GROUP_PAIRS)
+            step = 0
             for unit in range(UNITS_PER_GROUP):
                 works = []
                 for kq in range(UNIT_CLUSTERS):
                     k = unit * UNIT_CLUSTERS + kq
-                    std_T = transit.tile([P, HALVES, GROUP_ROWS], F32)
-                    add_per_dimension(std_T, sp_T, phi_sig_floor, g, k)
-                    work = slices.tile([P, GROUP_TILES, XD], F32)
-                    works.append((work, g, k))
-                    for pair in range(GROUP_PAIRS):
-                        std = banks.tile([P, 2, XD], F32)
-                        rows_to_partitions(std, std_T, 2 * pair * P)
-                        for two in range(2):
-                            j = 2 * pair + two
-                            nc.scalar.activation(
-                                out=work[:, j, :], in_=std[:, two, :], func=ACT.Ln,
-                                accum_out=sum_log[:, g * GROUP_TILES + j, k : k + 1],
-                            )
+                    works.append((log_of_std(g, k), g, k))
                     if unsummed:
                         sum_of_squares(*unsummed[kq])
-                for work, g, k in works:
-                    diff_T = transit.tile([P, HALVES, GROUP_ROWS], F32)
-                    add_per_dimension(diff_T, mu_T, neg_phi_mu, g, k)
-                    nc.scalar.activation(out=work[:], in_=work[:], func=ACT.Exp, scale=-1.0)
-                    for pair in range(GROUP_PAIRS):
-                        diff = banks.tile([P, 2, XD], F32)
-                        rows_to_partitions(diff, diff_T, 2 * pair * P)
-                        nc.vector.tensor_tensor(
-                            out=work[:, 2 * pair : 2 * pair + 2, :], in0=diff[:],
-                            in1=work[:, 2 * pair : 2 * pair + 2, :], op=ALU.mult,
-                        )
+                    if side_work[step] is not None:
+                        side_work[step]()
+                    step += 1
+                for work, g_of_work, k in works:
+                    scaled_difference(work, g_of_work, k)
+                    if side_work[step] is not None:
+                        side_work[step]()
+                    step += 1
                 unsummed = works
         for item in unsummed:
             sum_of_squares(*item)
@@ -266,6 +315,7 @@ def tile_deepgmm_pa_t_kernel(
         by_tile = stats[:].rearrange("p a k (j c) -> p a j k c", c=3)
         mean = by_tile[:, :, :, :, 1]
         spread = by_tile[:, :, :, :, 2]
+        z = const.tile([P, TILES, CLUSTERS], F32)
         z_pairs = z[:].rearrange("p (a j) k -> p a j k", j=2)
         nc.vector.tensor_tensor(out=z_pairs, in0=mean, in1=mean, op=ALU.mult)
         nc.vector.tensor_scalar(out=z[:], in0=z[:], scalar1=float(XD), scalar2=None, op0=ALU.mult)
@@ -276,11 +326,14 @@ def tile_deepgmm_pa_t_kernel(
         nc.vector.tensor_tensor(
             out=z[:], in0=z[:], in1=logits[:].unsqueeze(1).to_broadcast([P, TILES, CLUSTERS]), op=ALU.add
         )
+        z_max = const.tile([P, TILES], F32)
         nc.vector.tensor_reduce(out=z_max[:], in_=z[:], axis=AXIS.X, op=ALU.max)
         nc.vector.tensor_tensor(
             out=z[:], in0=z[:], in1=z_max[:].unsqueeze(2).to_broadcast([P, TILES, CLUSTERS]), op=ALU.subtract
         )
+        z_exp = const.tile([P, TILES, CLUSTERS], F32)
         nc.scalar.activation(out=z_exp[:], in_=z[:], func=ACT.Exp)
+        z_sum = const.tile([P, TILES], F32)
         nc.vector.tensor_reduce(out=z_sum[:], in_=z_exp[:], axis=AXIS.X, op=ALU.add)
         nc.scalar.activation(out=z_sum[:], in_=z_sum[:], func=ACT.Ln)
         nc.vector.tensor_tensor(

@@ -20,19 +20,17 @@ XD = 256
 HALVES = XD // P
 CLUSTERS = 16
 TILES = ROWS // P
-GROUP_TILES = 8
-GROUP_PAIRS = GROUP_TILES // 2
-GROUPS = TILES // GROUP_TILES
-GROUP_ROWS = GROUP_TILES * P
-UNIT_CLUSTERS = 8
-UNITS_PER_GROUP = CLUSTERS // UNIT_CLUSTERS
-MX_COLS = 512
-STEPS_PER_GROUP = 2 * CLUSTERS
-ENCODER_STAGES = GROUP_PAIRS + 1 + 2 * HALVES * (GROUP_ROWS // MX_COLS) + 5
-TRANSIT_BUFS = 3
-assert UNIT_CLUSTERS <= ENCODER_STAGES - 4 < 2 * UNIT_CLUSTERS
-assert 2 * UNIT_CLUSTERS <= ENCODER_STAGES - 2 < 3 * UNIT_CLUSTERS
+UNIT_TILES = 4
+UNIT_PAIRS = UNIT_TILES // 2
+UNITS = TILES // UNIT_TILES
+UNIT_ROWS = UNIT_TILES * P
 SIG_FLOOR = 1e-3
+LOG_2 = 0.6931471805599453
+LOG_BUFS = 22
+RATIO_BUFS = 14
+AUX_BANKS = 3
+SUM_BANKS = 3
+SUM_LAG = SUM_BANKS
 
 ROW_PHI_MU = 0
 ROW_PHI_SIG = CLUSTERS
@@ -67,34 +65,39 @@ def tile_deepgmm_pa_t_kernel(
     with ExitStack() as ctx:
         ctx.enter_context(tc.manual_schedule())
         const = ctx.enter_context(tc.tile_pool(name="const", bufs=1))
-        enc = ctx.enter_context(tc.tile_pool(name="enc", bufs=1))
-        latent = ctx.enter_context(tc.tile_pool(name="latent", bufs=2))
-        transit = ctx.enter_context(tc.tile_pool(name="transit", bufs=TRANSIT_BUFS))
-        slices = ctx.enter_context(tc.tile_pool(name="slices", bufs=UNIT_CLUSTERS + 2))
-        banks = ctx.enter_context(tc.psum_pool(name="banks", bufs=3))
+        enc = ctx.enter_context(tc.tile_pool(name="enc", bufs=2))
+        logs = ctx.enter_context(tc.tile_pool(name="logs", bufs=LOG_BUFS))
+        ratios = ctx.enter_context(tc.tile_pool(name="ratios", bufs=RATIO_BUFS))
+        banks = ctx.enter_context(tc.psum_pool(name="banks", bufs=AUX_BANKS))
 
         ident = const.tile([P, P], F32)
         masks.make_identity(nc, ident[:])
-        ones_col = const.tile([P, 1], F32)
-        nc.vector.memset(ones_col[:], 1.0)
         w_words = const.tile([P, 2, XD], U32, align_bytes=64)
         w_planes = const.tile([P, 2, XD], U8, align_bytes=64)
         nc.vector.memset(w_planes[:].rearrange("p w n -> p (w n)").bitcast(I32), 0)
         param_rows_bf = const.tile([P, XD], BF16)
         nc.vector.memset(param_rows_bf[:].bitcast(I32), 0)
+        zero_col = const.tile([P, 1], F32)
+        nc.vector.memset(zero_col[:], 0.0)
+        ones_col = const.tile([P, 1], F32)
+        nc.vector.memset(ones_col[:], 1.0)
+        half_col = const.tile([P, 1], F32)
+        nc.vector.tensor_scalar(
+            out=half_col[:], in0=zero_col[:], scalar1=-0.5 * LOG_2, scalar2=None, op0=ALU.add
+        )
+        warm_col = const.tile([P, 1], F32)
+        nc.scalar.activation(out=warm_col[:], in_=zero_col[:], func=ACT.Exp)
         logits_bf = const.tile([P, CLUSTERS], BF16)
+        be_mu_bf = const.tile([P, XD], BF16)
 
-        def load_y(g):
-            y_rows = enc.tile([P, GROUP_TILES, YD], BF16, name="y_rows")
-            nc.sync.dma_start(out=y_rows[:], in_=y_tiles[:, g * GROUP_TILES : (g + 1) * GROUP_TILES, :])
-            return y_rows
+        y_loaded = {}
 
-        y_loaded = {0: load_y(0)}
-        nc.sync.dma_start(out=param_rows_bf[ROW_PHI_MU : ROW_PHI_MU + CLUSTERS, :], in_=phi_mus)
-        nc.sync.dma_start(out=param_rows_bf[ROW_PHI_SIG : ROW_PHI_SIG + CLUSTERS, :], in_=phi_sigs)
-        nc.sync.dma_start(out=param_rows_bf[ROW_BE_MU : ROW_BE_MU + 1, :], in_=be_mu.unsqueeze(0))
-        nc.sync.dma_start(out=param_rows_bf[ROW_BE_SIG : ROW_BE_SIG + 1, :], in_=be_sig.unsqueeze(0))
-        for w, (words, scales) in enumerate(((We_mu_words, We_mu_scales), (We_sig_words, We_sig_scales))):
+        def load_y(u):
+            y_rows = enc.tile([P, UNIT_TILES, YD], BF16, name="y_rows", bufs=4)
+            nc.sync.dma_start(out=y_rows[:], in_=y_tiles[:, u * UNIT_TILES : (u + 1) * UNIT_TILES, :])
+            y_loaded[u] = y_rows
+
+        def load_weight(w, words, scales):
             nc.sync.dma_start(
                 out=w_words[:, w, :].bitcast(I32),
                 in_=words[0].rearrange("p n t -> p (n t)").bitcast(I32),
@@ -104,227 +107,335 @@ def tile_deepgmm_pa_t_kernel(
                     out=w_planes[32 * quadrant : 32 * quadrant + 4, w, :].bitcast(I32),
                     in_=scales[0, 4 * quadrant : 4 * quadrant + 4, :].bitcast(I32),
                 )
+
+        load_y(0)
+        nc.sync.dma_start(out=param_rows_bf[ROW_PHI_MU : ROW_PHI_MU + CLUSTERS, :], in_=phi_mus)
+        nc.sync.dma_start(out=param_rows_bf[ROW_PHI_SIG : ROW_PHI_SIG + CLUSTERS, :], in_=phi_sigs)
+        nc.sync.dma_start(out=param_rows_bf[ROW_BE_MU : ROW_BE_MU + 1, :], in_=be_mu.unsqueeze(0))
+        nc.sync.dma_start(out=param_rows_bf[ROW_BE_SIG : ROW_BE_SIG + 1, :], in_=be_sig.unsqueeze(0))
+        load_weight(1, We_sig_words, We_sig_scales)
+        load_y(1)
+        load_weight(0, We_mu_words, We_mu_scales)
+        load_y(2)
+        load_y(3)
+        nc.sync.dma_start(out=be_mu_bf[:], in_=be_mu.partition_broadcast(P))
         nc.sync.dma_start(out=logits_bf[:], in_=phi_logits.partition_broadcast(P))
 
-        param_rows = const.tile([P, XD], F32)
-        nc.vector.tensor_copy(out=param_rows[:], in_=param_rows_bf[:])
-        params_ps = banks.tile([P, HALVES, P], F32, tag="aux", bufs=2)
-        for h in range(HALVES):
-            nc.tensor.transpose(out=params_ps[:, h, :], in_=param_rows[:, h * P : (h + 1) * P], identity=ident[:])
         params = const.tile([P, HALVES, P], F32)
-        nc.vector.tensor_copy(out=params[:], in_=params_ps[:])
-        neg_phi_mu = const.tile([P, HALVES, CLUSTERS], F32)
-        nc.vector.tensor_scalar(
-            out=neg_phi_mu[:], in0=params[:, :, ROW_PHI_MU : ROW_PHI_MU + CLUSTERS],
-            scalar1=-1.0, scalar2=None, op0=ALU.mult,
-        )
-        phi_sig_floor = const.tile([P, HALVES, CLUSTERS], F32)
-        nc.vector.tensor_scalar(
-            out=phi_sig_floor[:], in0=params[:, :, ROW_PHI_SIG : ROW_PHI_SIG + CLUSTERS],
-            scalar1=SIG_FLOOR, scalar2=None, op0=ALU.add,
-        )
-        logits = const.tile([P, CLUSTERS], F32)
-        nc.vector.tensor_copy(out=logits[:], in_=logits_bf[:])
+        shift = const.tile([P, HALVES, CLUSTERS], F32)
+        spread = const.tile([P, HALVES, CLUSTERS], F32)
+        held = {}
 
-        sum_log = const.tile([P, TILES, CLUSTERS], F32)
-        stats = const.tile([P, TILES // 2, CLUSTERS, 6], F32)
+        def turn_params():
+            param_rows = const.tile([P, XD], F32)
+            nc.vector.tensor_copy(out=param_rows[:], in_=param_rows_bf[:])
+            params_ps = banks.tile([P, HALVES, P], F32, tag="aux", bufs=AUX_BANKS)
+            for h in range(HALVES):
+                nc.tensor.transpose(out=params_ps[:, h, :], in_=param_rows[:, h * P : (h + 1) * P], identity=ident[:])
+            held["params"] = params_ps
 
-        def rows_to_partitions(bank, source, pair):
+        def derive_params():
+            nc.vector.tensor_copy(out=params[:], in_=held["params"][:])
+            for h in range(HALVES):
+                nc.vector.tensor_scalar(
+                    out=shift[:, h, :], in0=params[:, h, ROW_PHI_MU : ROW_PHI_MU + CLUSTERS],
+                    scalar1=params[:, h, ROW_BE_MU : ROW_BE_MU + 1], scalar2=None, op0=ALU.subtract,
+                )
+            nc.vector.tensor_scalar(
+                out=spread[:], in0=params[:, :, ROW_PHI_SIG : ROW_PHI_SIG + CLUSTERS],
+                scalar1=SIG_FLOOR, scalar2=None, op0=ALU.add,
+            )
+
+        grouped = {}
+        codes = {}
+        planes = {}
+        pre_sig = {}
+        soft = {}
+        sp_T = {}
+        mu_ps = {}
+
+        def turn_y(u, pair):
+            y_words = y_loaded[u][:].rearrange("p j k -> p (j k)").bitcast(F32)
+            y_T = banks.tile([P, 2, 2 * P], F32, tag="aux", bufs=AUX_BANKS)
+            for two in range(2):
+                first_word = (2 * pair + two) * (YD // 2)
+                for w in range(2):
+                    nc.tensor.transpose(
+                        out=y_T[:, w, two * P : (two + 1) * P],
+                        in_=y_words[:, first_word + w : first_word + YD // 2 : 2],
+                        identity=ident[:],
+                    )
+            held["y", u, pair] = y_T
+
+        def group_y(u, pair):
+            if pair == 0:
+                grouped[u] = enc.tile([P, UNIT_ROWS * 4], BF16, name="grouped", bufs=2, align_bytes=64)
+            grouped_words = grouped[u][:].bitcast(F32).rearrange("p (n w) -> p n w", w=2)
+            nc.vector.tensor_copy(
+                out=grouped_words[:, 2 * pair * P : (2 * pair + 2) * P, :],
+                in_=held["y", u, pair][:].rearrange("p w n -> p n w"),
+            )
+
+        def quantise(u):
+            codes[u] = enc.tile([P, UNIT_ROWS], U32, name="y_codes", bufs=4, align_bytes=64)
+            planes[u] = enc.tile([P, UNIT_ROWS], U8, name="y_planes", bufs=4, align_bytes=64)
+            nc.vector.quantize_mx(out=codes[u][:].bitcast(FP8X4), scales=planes[u][:], in_=grouped[u][:])
+
+        def product(acc, w, h, u):
+            nc.tensor.matmul_mx(
+                out=acc[:],
+                lhsT=w_words[:, w, h * P : (h + 1) * P].bitcast(FP8X4),
+                lhsT_scale=w_planes[:, w, h * P : (h + 1) * P],
+                rhs=codes[u][:].bitcast(FP8X4),
+                rhs_scale=planes[u][:],
+                start=True,
+                stop=True,
+            )
+
+        def sig_product(u, h):
+            acc = banks.tile([P, UNIT_ROWS], F32, tag="aux", bufs=AUX_BANKS)
+            product(acc, 1, h, u)
+            held["sig", u, h] = acc
+
+        def sig_bias(u, h):
+            if h == 0:
+                pre_sig[u] = enc.tile([P, HALVES, UNIT_ROWS], F32, name="pre_sig", bufs=2)
+            nc.vector.tensor_scalar(
+                out=pre_sig[u][:, h, :], in0=held["sig", u, h][:],
+                scalar1=params[:, h, ROW_BE_SIG : ROW_BE_SIG + 1], scalar2=None, op0=ALU.add,
+            )
+
+        def minus_abs(u):
+            soft[u] = enc.tile([P, HALVES, UNIT_ROWS], F32, name="soft", bufs=2)
+            nc.vector.scalar_tensor_tensor(
+                out=soft[u][:], in0=pre_sig[u][:], scalar=-1.0, in1=pre_sig[u][:], op0=ALU.mult, op1=ALU.min
+            )
+
+        def soft_exp(u):
+            nc.scalar.activation(out=soft[u][:], in_=soft[u][:], func=ACT.Exp)
+
+        def soft_log(u):
+            nc.scalar.activation(out=soft[u][:], in_=soft[u][:], func=ACT.Ln, bias=ones_col[:])
+
+        def softplus(u):
+            sp_T[u] = enc.tile([P, HALVES, UNIT_ROWS], F32, name="sp_T", bufs=2)
+            nc.vector.scalar_tensor_tensor(
+                out=sp_T[u][:], in0=pre_sig[u][:], scalar=0.0, in1=soft[u][:], op0=ALU.max, op1=ALU.add
+            )
+
+        def mu_product(u):
+            for h in range(HALVES):
+                acc = banks.tile([P, UNIT_ROWS], F32, tag="mu", bufs=HALVES)
+                product(acc, 0, h, u)
+                mu_ps[u, h] = acc
+
+        def store(dram, u, pair, out_rows):
+            first_tile = u * UNIT_TILES + 2 * pair
+            nc.sync.dma_start(out=dram[:, first_tile : first_tile + 2, :], in_=out_rows[:])
+
+        def mu_rows(u, pair):
+            bank = banks.tile([P, 2, XD], F32, tag="aux", bufs=AUX_BANKS)
+            for two in range(2):
+                cols = slice((2 * pair + two) * P, (2 * pair + two + 1) * P)
+                nc.tensor.matmul_mx(
+                    out=bank[:, two, :],
+                    lhsT=codes[u][:, cols].bitcast(FP8X4),
+                    lhsT_scale=planes[u][:, cols],
+                    rhs=w_words[:, 0, :].bitcast(FP8X4),
+                    rhs_scale=w_planes[:, 0, :],
+                    start=True,
+                    stop=True,
+                )
+            held["mu", u, pair] = bank
+
+        def store_mu(u, pair):
+            out_rows = enc.tile([P, 2, XD], F32, name="out_rows", bufs=4)
+            nc.vector.tensor_tensor(
+                out=out_rows[:], in0=held["mu", u, pair][:],
+                in1=be_mu_rows[:].unsqueeze(1).to_broadcast([P, 2, XD]), op=ALU.add,
+            )
+            store(mu_out, u, pair, out_rows)
+
+        def sig_rows(u, pair):
+            bank = banks.tile([P, 2, XD], F32, tag="aux", bufs=AUX_BANKS)
             for two in range(2):
                 first = (2 * pair + two) * P
                 for h in range(HALVES):
                     nc.tensor.transpose(
-                        out=bank[:, two, h * P : (h + 1) * P], in_=source[:, h, first : first + P], identity=ident[:]
+                        out=bank[:, two, h * P : (h + 1) * P], in_=sp_T[u][:, h, first : first + P], identity=ident[:]
                     )
+            held["sp", u, pair] = bank
 
-        mu_T = {}
-        sp_T = {}
+        def store_sig(u, pair):
+            out_rows = enc.tile([P, 2, XD], F32, name="out_rows", bufs=4)
+            nc.vector.tensor_scalar(
+                out=out_rows[:], in0=held["sp", u, pair][:], scalar1=SIG_FLOOR, scalar2=None, op0=ALU.add
+            )
+            store(sig_out, u, pair, out_rows)
 
-        def encoder_stages(g):
-            tiles = {}
+        log_of = {}
+        ratio_of = {}
+        sums = const.tile([P, TILES, CLUSTERS], F32)
 
-            def turn_y(pair):
-                if pair == 0:
-                    tiles["grouped"] = enc.tile([P, GROUP_ROWS * 4], BF16, name="grouped", align_bytes=64)
-                y_words = y_loaded[g][:].rearrange("p j k -> p (j k)").bitcast(F32)
-                grouped_words = tiles["grouped"][:].bitcast(F32).rearrange("p (n u) -> p n u", u=2)
-                y_T = banks.tile([P, 2, 2 * P], F32, tag="aux", bufs=2)
-                for two in range(2):
-                    first_word = (2 * pair + two) * (YD // 2)
-                    for u in range(2):
-                        nc.tensor.transpose(
-                            out=y_T[:, u, two * P : (two + 1) * P],
-                            in_=y_words[:, first_word + u : first_word + YD // 2 : 2],
-                            identity=ident[:],
-                        )
-                nc.vector.tensor_copy(
-                    out=grouped_words[:, 2 * pair * P : (2 * pair + 2) * P, :],
-                    in_=y_T[:].rearrange("p u n -> p n u"),
-                )
-
-            def quantise():
-                if g + 1 < GROUPS:
-                    y_loaded[g + 1] = load_y(g + 1)
-                tiles["codes"] = enc.tile([P, GROUP_ROWS], U32, name="y_codes", align_bytes=64)
-                tiles["scales"] = enc.tile([P, GROUP_ROWS], U8, name="y_scales", align_bytes=64)
-                nc.vector.quantize_mx(
-                    out=tiles["codes"][:].bitcast(FP8X4), scales=tiles["scales"][:], in_=tiles["grouped"][:]
-                )
-                tiles["pre_sig"] = enc.tile([P, HALVES, GROUP_ROWS], F32, name="pre_sig")
-                mu_T[g] = latent.tile([P, HALVES, GROUP_ROWS], F32, name="mu_T")
-
-            def product(w, h, c):
-                cols = slice(c * MX_COLS, (c + 1) * MX_COLS)
-                acc = banks.tile([P, MX_COLS], F32, tag="aux", bufs=2)
-                nc.tensor.matmul_mx(
-                    out=acc[:],
-                    lhsT=w_words[:, w, h * P : (h + 1) * P].bitcast(FP8X4),
-                    lhsT_scale=w_planes[:, w, h * P : (h + 1) * P],
-                    rhs=tiles["codes"][:, cols].bitcast(FP8X4),
-                    rhs_scale=tiles["scales"][:, cols],
-                    start=True,
-                    stop=True,
-                )
-                target, bias_row = ((mu_T[g], ROW_BE_MU), (tiles["pre_sig"], ROW_BE_SIG))[w]
-                nc.vector.tensor_scalar(
-                    out=target[:, h, cols], in0=acc[:],
-                    scalar1=params[:, h, bias_row : bias_row + 1], scalar2=None, op0=ALU.add,
-                )
-
-            def minus_abs():
-                tiles["soft"] = enc.tile([P, HALVES, GROUP_ROWS], F32, name="soft")
-                nc.vector.scalar_tensor_tensor(
-                    out=tiles["soft"][:], in0=tiles["pre_sig"][:], scalar=-1.0, in1=tiles["pre_sig"][:],
-                    op0=ALU.mult, op1=ALU.min,
-                )
-
-            def soft_exp():
-                nc.scalar.activation(out=tiles["soft"][:], in_=tiles["soft"][:], func=ACT.Exp)
-
-            def soft_log():
-                nc.scalar.activation(out=tiles["soft"][:], in_=tiles["soft"][:], func=ACT.Ln, bias=ones_col[:])
-
-            def softplus():
-                sp_T[g] = latent.tile([P, HALVES, GROUP_ROWS], F32, name="sp_T")
-                nc.vector.scalar_tensor_tensor(
-                    out=sp_T[g][:], in0=tiles["pre_sig"][:], scalar=0.0, in1=tiles["soft"][:],
-                    op0=ALU.max, op1=ALU.add,
-                )
-
-            stages = [lambda pair=pair: turn_y(pair) for pair in range(GROUP_PAIRS)]
-            stages.append(quantise)
-            for w in (1, 0):
-                stages.extend(
-                    lambda w=w, h=h, c=c: product(w, h, c)
-                    for h in range(HALVES)
-                    for c in range(GROUP_ROWS // MX_COLS)
-                )
-                if w == 1:
-                    stages.append(minus_abs)
-            stages.append(None)
-            stages.append(soft_exp)
-            stages.append(soft_log)
-            stages.append(softplus)
-            return stages
-
-        def output_stages(g):
-            def emit(source, floor, dram, pair):
-                turned = banks.tile([P, 2, XD], F32, tag="aux", bufs=2)
-                rows_to_partitions(turned, source, pair)
-                out_rows = enc.tile([P, 2, XD], F32, name="out_rows", bufs=3)
-                nc.vector.tensor_scalar(out=out_rows[:], in0=turned[:], scalar1=floor, scalar2=None, op0=ALU.add)
-                first_tile = g * GROUP_TILES + 2 * pair
-                nc.sync.dma_start(out=dram[:, first_tile : first_tile + 2, :], in_=out_rows[:])
-
-            return [
-                lambda source=source, floor=floor, dram=dram, pair=pair: emit(source, floor, dram, pair)
-                for source, floor, dram in ((mu_T[g], 0.0, mu_out), (sp_T[g], SIG_FLOOR, sig_out))
-                for pair in range(GROUP_PAIRS)
-            ]
-
-        def add_per_dimension(out_tile, source, column, k):
+        def log_std(u, k):
+            log_t = logs.tile([P, HALVES, UNIT_ROWS], F32, name="log_t")
             for h in range(HALVES):
-                nc.gpsimd.tensor_scalar(
-                    out=out_tile[:, h, :], in0=source[:, h, :],
-                    scalar1=column[:, h, k : k + 1], scalar2=1.0, op0=ALU.add, op1=ALU.mult,
+                nc.scalar.activation(
+                    out=log_t[:, h, :], in_=sp_T[u][:, h, :], func=ACT.Ln, bias=spread[:, h, k : k + 1]
+                )
+            log_of[u, k] = log_t
+
+        def inverse_std(u, k):
+            ratio = ratios.tile([P, HALVES, UNIT_ROWS], F32, name="ratio")
+            nc.scalar.activation(out=ratio[:], in_=log_of[u, k][:], func=ACT.Exp, scale=-1.0, bias=half_col[:])
+            ratio_of[u, k] = ratio
+
+        def scaled_difference(u, k):
+            for h in range(HALVES):
+                nc.vector.scalar_tensor_tensor(
+                    out=ratio_of[u, k][:, h, :], in0=mu_ps[u, h][:], scalar=shift[:, h, k : k + 1],
+                    in1=ratio_of[u, k][:, h, :], op0=ALU.subtract, op1=ALU.mult,
                 )
 
-        def log_of_std(g, k):
-            std_T = transit.tile([P, HALVES, GROUP_ROWS], F32, name="std_T")
-            add_per_dimension(std_T, sp_T[g], phi_sig_floor, k)
-            work = slices.tile([P, GROUP_TILES, XD], F32, name="work")
-            for pair in range(GROUP_PAIRS):
-                std = banks.tile([P, 2, XD], F32, name="std")
-                rows_to_partitions(std, std_T, pair)
-                for two in range(2):
-                    j = 2 * pair + two
-                    nc.scalar.activation(
-                        out=work[:, j, :], in_=std[:, two, :], func=ACT.Ln,
-                        accum_out=sum_log[:, g * GROUP_TILES + j, k : k + 1],
+        def square(u, k):
+            ratio = ratio_of[u, k]
+            if u == UNITS - 1 and k % 2 == 1:
+                nc.scalar.activation(out=ratio[:], in_=ratio[:], func=ACT.Square)
+            else:
+                nc.gpsimd.tensor_tensor(out=ratio[:], in0=ratio[:], in1=ratio[:], op=ALU.mult)
+
+        def add_up(u, k):
+            bank = banks.tile([P, UNIT_TILES, P], F32, tag="sum", bufs=SUM_BANKS)
+            for j in range(UNIT_TILES):
+                parts = [(source, h) for source in (log_of[u, k], ratio_of[u, k]) for h in range(HALVES)]
+                for n, (source, h) in enumerate(parts):
+                    nc.tensor.matmul(
+                        out=bank[:, j, :], lhsT=source[:, h, j * P : (j + 1) * P], rhs=ident[:],
+                        is_transpose=True, start=(n == 0), stop=(n == len(parts) - 1),
                     )
-            return work
+            held["sum", u, k] = bank
 
-        def scaled_difference(work, g, k):
-            diff_T = transit.tile([P, HALVES, GROUP_ROWS], F32, name="diff_T")
-            add_per_dimension(diff_T, mu_T[g], neg_phi_mu, k)
-            nc.scalar.activation(out=work[:], in_=work[:], func=ACT.Exp, scale=-1.0)
-            for pair in range(GROUP_PAIRS):
-                diff = banks.tile([P, 2, XD], F32, name="diff")
-                rows_to_partitions(diff, diff_T, pair)
-                nc.vector.tensor_tensor(
-                    out=work[:, 2 * pair : 2 * pair + 2, :], in0=diff[:],
-                    in1=work[:, 2 * pair : 2 * pair + 2, :], op=ALU.mult,
-                )
+        def sum_columns(step):
+            u, k = divmod(step, CLUSTERS)
+            nc.vector.tensor_reduce(
+                out=sums[:, u * UNIT_TILES : (u + 1) * UNIT_TILES, k], in_=held["sum", u, k][:],
+                axis=AXIS.X, op=ALU.add,
+            )
 
-        def sum_of_squares(work, g, k):
-            for pair in range(GROUP_PAIRS):
-                nc.vector.bn_stats(
-                    out=stats[:, g * GROUP_PAIRS + pair, k, :],
-                    in_=work[:, 2 * pair : 2 * pair + 2, :].rearrange("p j d -> p d j"),
-                )
+        turn_y(0, 0)
+        turn_y(0, 1)
+        turn_params()
+        group_y(0, 0)
+        group_y(0, 1)
+        derive_params()
+        quantise(0)
+        turn_y(1, 0)
+        turn_y(1, 1)
+        sig_product(0, 0)
+        group_y(1, 0)
+        group_y(1, 1)
+        sig_bias(0, 0)
+        sig_product(0, 1)
+        sig_bias(0, 1)
+        minus_abs(0)
+        soft_exp(0)
+        quantise(1)
+        sig_product(1, 0)
+        sig_product(1, 1)
+        sig_bias(1, 0)
+        sig_bias(1, 1)
+        minus_abs(1)
+        soft_exp(1)
+        soft_log(0)
+        softplus(0)
+        mu_product(0)
+        be_mu_rows = const.tile([P, XD], F32)
+        nc.vector.tensor_copy(out=be_mu_rows[:], in_=be_mu_bf[:])
+        logits = const.tile([P, CLUSTERS], F32)
+        nc.vector.tensor_copy(out=logits[:], in_=logits_bf[:])
 
-        for stage in encoder_stages(0):
-            if stage is not None:
-                stage()
+        def behind_the_first_logs():
+            turn_y(2, 0)
+            turn_y(2, 1)
+            mu_rows(0, 0)
+            group_y(2, 0)
+            group_y(2, 1)
+            store_mu(0, 0)
+            mu_rows(0, 1)
+            mu_rows(1, 0)
+            mu_rows(1, 1)
+            quantise(2)
+            store_mu(0, 1)
+            store_mu(1, 0)
+            store_mu(1, 1)
+            sig_rows(0, 0)
+            sig_rows(0, 1)
+            sig_product(2, 0)
+            store_sig(0, 0)
+            store_sig(0, 1)
+            sig_product(2, 1)
 
-        unsummed = []
-        for g in range(GROUPS):
-            side_work = encoder_stages(g + 1) if g + 1 < GROUPS else [None] * ENCODER_STAGES
-            assert len(side_work) == ENCODER_STAGES
-            side_work = side_work + output_stages(g) + [None] * (STEPS_PER_GROUP - ENCODER_STAGES - 2 * GROUP_PAIRS)
-            step = 0
-            for unit in range(UNITS_PER_GROUP):
-                works = []
-                for kq in range(UNIT_CLUSTERS):
-                    k = unit * UNIT_CLUSTERS + kq
-                    works.append((log_of_std(g, k), g, k))
-                    if unsummed:
-                        sum_of_squares(*unsummed[kq])
-                    if side_work[step] is not None:
-                        side_work[step]()
-                    step += 1
-                for work, g_of_work, k in works:
-                    scaled_difference(work, g_of_work, k)
-                    if side_work[step] is not None:
-                        side_work[step]()
-                    step += 1
-                unsummed = works
-        for item in unsummed:
-            sum_of_squares(*item)
+        def side_work(u):
+            vector = {}
+            tensor = {}
+            if u + 4 < UNITS:
+                vector[0] = [lambda: load_y(u + 4)]
+            if u + 2 < UNITS:
+                vector.setdefault(0, []).append(lambda: sig_bias(u + 2, 0))
+                vector[1] = [lambda: sig_bias(u + 2, 1)]
+                vector[2] = [lambda: minus_abs(u + 2)]
+                tensor[2] = [lambda: mu_rows(u + 2, 0)]
+                tensor[3] = [lambda: mu_rows(u + 2, 1)]
+                vector[5] = [lambda: store_mu(u + 2, 0)]
+                vector[6] = [lambda: store_mu(u + 2, 1)]
+            if u + 1 < UNITS:
+                vector[4] = [lambda: softplus(u + 1)]
+                tensor[5] = [lambda: sig_rows(u + 1, 0)]
+                tensor[6] = [lambda: sig_rows(u + 1, 1)]
+                vector[8] = [lambda: store_sig(u + 1, 0)]
+                vector[9] = [lambda: store_sig(u + 1, 1)]
+            if u + 3 < UNITS:
+                tensor[8] = [lambda: turn_y(u + 3, 0)]
+                tensor[9] = [lambda: turn_y(u + 3, 1)]
+                vector[11] = [lambda: group_y(u + 3, 0)]
+                vector[12] = [lambda: group_y(u + 3, 1)]
+                vector[13] = [lambda: quantise(u + 3)]
+                tensor[14] = [lambda: sig_product(u + 3, 0)]
+                tensor[15] = [lambda: sig_product(u + 3, 1)]
+            if u + 1 < UNITS:
+                tensor.setdefault(15, []).append(lambda: mu_product(u + 1))
+            return vector, tensor
 
-        by_tile = stats[:].rearrange("p a k (j c) -> p a j k c", c=3)
-        mean = by_tile[:, :, :, :, 1]
-        spread = by_tile[:, :, :, :, 2]
+        for u in range(UNITS):
+            for k in range(CLUSTERS):
+                log_std(u, k)
+            if u + 1 < UNITS:
+                soft_log(u + 1)
+            if u == 0:
+                behind_the_first_logs()
+            vector_side, tensor_side = side_work(u)
+            for j in range(CLUSTERS):
+                for k in range(0 if j == 0 else j + 2, min(j + 3, CLUSTERS)):
+                    inverse_std(u, k)
+                if j == CLUSTERS - 3 and u + 2 < UNITS:
+                    soft_exp(u + 2)
+                for k in range(0 if j == 0 else j + 1, min(j + 2, CLUSTERS)):
+                    scaled_difference(u, k)
+                if u * CLUSTERS + j >= SUM_LAG:
+                    sum_columns(u * CLUSTERS + j - SUM_LAG)
+                for stage in vector_side.get(j, []):
+                    stage()
+                square(u, j)
+                for stage in tensor_side.get(j, []):
+                    stage()
+                add_up(u, j)
+        for step in range(UNITS * CLUSTERS - SUM_LAG, UNITS * CLUSTERS):
+            sum_columns(step)
+
         z = const.tile([P, TILES, CLUSTERS], F32)
-        z_pairs = z[:].rearrange("p (a j) k -> p a j k", j=2)
-        nc.vector.tensor_tensor(out=z_pairs, in0=mean, in1=mean, op=ALU.mult)
-        nc.vector.tensor_scalar(out=z[:], in0=z[:], scalar1=float(XD), scalar2=None, op0=ALU.mult)
-        nc.vector.tensor_tensor(out=z_pairs, in0=z_pairs, in1=spread, op=ALU.add)
         nc.vector.scalar_tensor_tensor(
-            out=z[:], in0=z[:], scalar=-0.5, in1=sum_log[:], op0=ALU.mult, op1=ALU.subtract
-        )
-        nc.vector.tensor_tensor(
-            out=z[:], in0=z[:], in1=logits[:].unsqueeze(1).to_broadcast([P, TILES, CLUSTERS]), op=ALU.add
+            out=z[:], in0=sums[:], scalar=-1.0, in1=logits[:].unsqueeze(1).to_broadcast([P, TILES, CLUSTERS]),
+            op0=ALU.mult, op1=ALU.add,
         )
         z_max = const.tile([P, TILES], F32)
         nc.vector.tensor_reduce(out=z_max[:], in_=z[:], axis=AXIS.X, op=ALU.max)

@@ -30,6 +30,7 @@ LOG_BUFS = 22
 RATIO_BUFS = 14
 AUX_BANKS = 3
 SUM_BANKS = 3
+VECTOR_SQUARES = (4, 9, 14)
 SUM_LAG = SUM_BANKS
 
 ROW_PHI_MU = 0
@@ -85,6 +86,8 @@ def tile_deepgmm_pa_t_kernel(
         nc.vector.tensor_scalar(
             out=half_col[:], in0=zero_col[:], scalar1=-0.5 * LOG_2, scalar2=None, op0=ALU.add
         )
+        full_col = const.tile([P, 1], F32)
+        nc.vector.tensor_scalar(out=full_col[:], in0=zero_col[:], scalar1=-LOG_2, scalar2=None, op0=ALU.add)
         warm_col = const.tile([P, 1], F32)
         nc.scalar.activation(out=warm_col[:], in_=zero_col[:], func=ACT.Exp)
         logits_bf = const.tile([P, CLUSTERS], BF16)
@@ -287,7 +290,10 @@ def tile_deepgmm_pa_t_kernel(
 
         def inverse_std(u, k):
             ratio = ratios.tile([P, HALVES, UNIT_ROWS], F32, name="ratio")
-            nc.scalar.activation(out=ratio[:], in_=log_of[u, k][:], func=ACT.Exp, scale=-1.0, bias=half_col[:])
+            if k in VECTOR_SQUARES:
+                nc.scalar.activation(out=ratio[:], in_=log_of[u, k][:], func=ACT.Exp, scale=-2.0, bias=full_col[:])
+            else:
+                nc.scalar.activation(out=ratio[:], in_=log_of[u, k][:], func=ACT.Exp, scale=-1.0, bias=half_col[:])
             ratio_of[u, k] = ratio
 
         def scaled_difference(u, k):
@@ -299,7 +305,9 @@ def tile_deepgmm_pa_t_kernel(
 
         def square(u, k):
             ratio = ratio_of[u, k]
-            if u == UNITS - 1 and k % 2 == 1:
+            if k in VECTOR_SQUARES:
+                scaled_difference(u, k)
+            elif u == UNITS - 1 and k % 2 == 1:
                 nc.scalar.activation(out=ratio[:], in_=ratio[:], func=ACT.Square)
             else:
                 nc.gpsimd.tensor_tensor(out=ratio[:], in0=ratio[:], in1=ratio[:], op=ALU.mult)

@@ -152,7 +152,7 @@ def tile_deepgmm_pa_t_kernel(
         grouped = {}
         codes = {}
         planes = {}
-        pre_sig = {}
+        positive = {}
         soft = {}
         sp_T = {}
         mu_ps = {}
@@ -200,31 +200,35 @@ def tile_deepgmm_pa_t_kernel(
             product(acc, 1, h, u)
             held["sig", u, h] = acc
 
-        def sig_bias(u, h):
+        def positive_part(u, h):
             if h == 0:
-                pre_sig[u] = enc.tile([P, HALVES, UNIT_ROWS], F32, name="pre_sig", bufs=2)
+                positive[u] = enc.tile([P, HALVES, UNIT_ROWS], F32, name="positive", bufs=2)
             nc.vector.tensor_scalar(
-                out=pre_sig[u][:, h, :], in0=held["sig", u, h][:],
-                scalar1=params[:, h, ROW_BE_SIG : ROW_BE_SIG + 1], scalar2=None, op0=ALU.add,
+                out=positive[u][:, h, :], in0=held["sig", u, h][:],
+                scalar1=params[:, h, ROW_BE_SIG : ROW_BE_SIG + 1], scalar2=0.0, op0=ALU.add, op1=ALU.max,
             )
 
-        def minus_abs(u):
-            soft[u] = enc.tile([P, HALVES, UNIT_ROWS], F32, name="soft", bufs=2)
+        def minus_abs(u, h):
+            if h == 0:
+                soft[u] = enc.tile([P, HALVES, UNIT_ROWS], F32, name="soft", bufs=2)
             nc.vector.scalar_tensor_tensor(
-                out=soft[u][:], in0=pre_sig[u][:], scalar=-1.0, in1=pre_sig[u][:], op0=ALU.mult, op1=ALU.min
+                out=soft[u][:, h, :], in0=positive[u][:, h, :], scalar=-2.0, in1=held["sig", u, h][:],
+                op0=ALU.mult, op1=ALU.add,
             )
 
         def soft_exp(u):
-            nc.scalar.activation(out=soft[u][:], in_=soft[u][:], func=ACT.Exp)
+            for h in range(HALVES):
+                nc.scalar.activation(
+                    out=soft[u][:, h, :], in_=soft[u][:, h, :], func=ACT.Exp,
+                    bias=params[:, h, ROW_BE_SIG : ROW_BE_SIG + 1],
+                )
 
         def soft_log(u):
             nc.scalar.activation(out=soft[u][:], in_=soft[u][:], func=ACT.Ln, bias=ones_col[:])
 
-        def softplus(u):
+        def softplus(u, engine):
             sp_T[u] = enc.tile([P, HALVES, UNIT_ROWS], F32, name="sp_T", bufs=2)
-            nc.vector.scalar_tensor_tensor(
-                out=sp_T[u][:], in0=pre_sig[u][:], scalar=0.0, in1=soft[u][:], op0=ALU.max, op1=ALU.add
-            )
+            engine.tensor_tensor(out=sp_T[u][:], in0=positive[u][:], in1=soft[u][:], op=ALU.add)
 
         def mu_product(u):
             for h in range(HALVES):
@@ -342,20 +346,22 @@ def tile_deepgmm_pa_t_kernel(
         sig_product(0, 0)
         group_y(1, 0)
         group_y(1, 1)
-        sig_bias(0, 0)
         sig_product(0, 1)
-        sig_bias(0, 1)
-        minus_abs(0)
+        positive_part(0, 0)
+        positive_part(0, 1)
+        minus_abs(0, 0)
+        minus_abs(0, 1)
         soft_exp(0)
         quantise(1)
         sig_product(1, 0)
         sig_product(1, 1)
-        sig_bias(1, 0)
-        sig_bias(1, 1)
-        minus_abs(1)
+        positive_part(1, 0)
+        positive_part(1, 1)
+        minus_abs(1, 0)
+        minus_abs(1, 1)
         soft_exp(1)
         soft_log(0)
-        softplus(0)
+        softplus(0, nc.vector)
         mu_product(0)
         be_mu_rows = const.tile([P, XD], F32)
         nc.vector.tensor_copy(out=be_mu_rows[:], in_=be_mu_bf[:])
@@ -389,15 +395,15 @@ def tile_deepgmm_pa_t_kernel(
             if u + 4 < UNITS:
                 vector[0] = [lambda: load_y(u + 4)]
             if u + 2 < UNITS:
-                vector.setdefault(0, []).append(lambda: sig_bias(u + 2, 0))
-                vector[1] = [lambda: sig_bias(u + 2, 1)]
-                vector[2] = [lambda: minus_abs(u + 2)]
+                vector.setdefault(0, []).append(lambda: positive_part(u + 2, 0))
+                vector[1] = [lambda: positive_part(u + 2, 1)]
+                vector[2] = [lambda: minus_abs(u + 2, 0), lambda: minus_abs(u + 2, 1)]
                 tensor[2] = [lambda: mu_rows(u + 2, 0)]
                 tensor[3] = [lambda: mu_rows(u + 2, 1)]
                 vector[5] = [lambda: store_mu(u + 2, 0)]
                 vector[6] = [lambda: store_mu(u + 2, 1)]
             if u + 1 < UNITS:
-                vector[4] = [lambda: softplus(u + 1)]
+                vector[4] = [lambda: softplus(u + 1, nc.gpsimd)]
                 tensor[5] = [lambda: sig_rows(u + 1, 0)]
                 tensor[6] = [lambda: sig_rows(u + 1, 1)]
                 vector[8] = [lambda: store_sig(u + 1, 0)]

@@ -26,11 +26,12 @@ UNITS = TILES // UNIT_TILES
 UNIT_ROWS = UNIT_TILES * P
 SIG_FLOOR = 1e-3
 LOG_2 = 0.6931471805599453
-LOG_BUFS = 22
-RATIO_BUFS = 14
+LOG_BUFS = 20
+RATIO_BUFS = 13
 AUX_BANKS = 3
 SUM_BANKS = 3
-VECTOR_SQUARES = (4, 9, 14)
+PAIRED = (15,)
+VECTOR_SQUARES = (3, 8, 13)
 SUM_LAG = SUM_BANKS
 
 ROW_PHI_MU = 0
@@ -203,10 +204,16 @@ def tile_deepgmm_pa_t_kernel(
         def positive_part(u, h):
             if h == 0:
                 positive[u] = enc.tile([P, HALVES, UNIT_ROWS], F32, name="positive", bufs=2)
-            nc.vector.tensor_scalar(
-                out=positive[u][:, h, :], in0=held["sig", u, h][:],
-                scalar1=params[:, h, ROW_BE_SIG : ROW_BE_SIG + 1], scalar2=0.0, op0=ALU.add, op1=ALU.max,
-            )
+            if u < 2:
+                nc.scalar.activation(
+                    out=positive[u][:, h, :], in_=held["sig", u, h][:], func=ACT.Relu,
+                    bias=params[:, h, ROW_BE_SIG : ROW_BE_SIG + 1],
+                )
+            else:
+                nc.vector.tensor_scalar(
+                    out=positive[u][:, h, :], in0=held["sig", u, h][:],
+                    scalar1=params[:, h, ROW_BE_SIG : ROW_BE_SIG + 1], scalar2=0.0, op0=ALU.add, op1=ALU.max,
+                )
 
         def minus_abs(u, h):
             if h == 0:
@@ -284,7 +291,38 @@ def tile_deepgmm_pa_t_kernel(
         ratio_of = {}
         sums = const.tile([P, TILES, CLUSTERS], F32)
 
+        def squarer(u, k):
+            if u == UNITS - 1:
+                return "scalar" if k % 2 == 1 else "gpsimd"
+            return "vector" if k in VECTOR_SQUARES else "gpsimd"
+
+        def pair_product(u, k):
+            swapped = ratios.tile([P, HALVES, UNIT_ROWS], F32, name="swapped", bufs=2 * len(PAIRED))
+            for h in range(HALVES):
+                nc.gpsimd.tensor_scalar(
+                    out=swapped[:, h, :], in0=sp_T[u][:, 1 - h, :],
+                    scalar1=spread[:, 1 - h, k : k + 1], scalar2=1.0, op0=ALU.add, op1=ALU.mult,
+                )
+            pair_log = logs.tile([P, UNIT_ROWS], F32, name="pair_log", bufs=2 * len(PAIRED))
+            nc.gpsimd.tensor_tensor(out=pair_log[:], in0=swapped[:, 0, :], in1=swapped[:, 1, :], op=ALU.mult)
+            ratio_of[u, k] = swapped
+            log_of[u, k] = pair_log
+
+        def pair_inverse(u, k):
+            inverse = ratios.tile([P, UNIT_ROWS], F32, name="inverse", bufs=2 * len(PAIRED))
+            nc.scalar.activation(out=inverse[:], in_=log_of[u, k][:], func=ACT.Exp, scale=-1.0, bias=half_col[:])
+            held["inverse", u, k] = inverse
+
+        def pair_ratio(u, k):
+            nc.gpsimd.tensor_tensor(
+                out=ratio_of[u, k][:], in0=ratio_of[u, k][:],
+                in1=held["inverse", u, k][:].unsqueeze(1).to_broadcast([P, HALVES, UNIT_ROWS]), op=ALU.mult,
+            )
+
         def log_std(u, k):
+            if k in PAIRED:
+                nc.scalar.activation(out=log_of[u, k][:], in_=log_of[u, k][:], func=ACT.Ln)
+                return
             log_t = logs.tile([P, HALVES, UNIT_ROWS], F32, name="log_t")
             for h in range(HALVES):
                 nc.scalar.activation(
@@ -293,8 +331,10 @@ def tile_deepgmm_pa_t_kernel(
             log_of[u, k] = log_t
 
         def inverse_std(u, k):
+            if k in PAIRED:
+                return
             ratio = ratios.tile([P, HALVES, UNIT_ROWS], F32, name="ratio")
-            if k in VECTOR_SQUARES:
+            if squarer(u, k) == "vector":
                 nc.scalar.activation(out=ratio[:], in_=log_of[u, k][:], func=ACT.Exp, scale=-2.0, bias=full_col[:])
             else:
                 nc.scalar.activation(out=ratio[:], in_=log_of[u, k][:], func=ACT.Exp, scale=-1.0, bias=half_col[:])
@@ -309,9 +349,9 @@ def tile_deepgmm_pa_t_kernel(
 
         def square(u, k):
             ratio = ratio_of[u, k]
-            if k in VECTOR_SQUARES:
+            if squarer(u, k) == "vector":
                 scaled_difference(u, k)
-            elif u == UNITS - 1 and k % 2 == 1:
+            elif squarer(u, k) == "scalar":
                 nc.scalar.activation(out=ratio[:], in_=ratio[:], func=ACT.Square)
             else:
                 nc.gpsimd.tensor_tensor(out=ratio[:], in0=ratio[:], in1=ratio[:], op=ALU.mult)
@@ -319,10 +359,15 @@ def tile_deepgmm_pa_t_kernel(
         def add_up(u, k):
             bank = banks.tile([P, UNIT_TILES, P], F32, tag="sum", bufs=SUM_BANKS)
             for j in range(UNIT_TILES):
-                parts = [(source, h) for source in (log_of[u, k], ratio_of[u, k]) for h in range(HALVES)]
-                for n, (source, h) in enumerate(parts):
+                rows = slice(j * P, (j + 1) * P)
+                parts = [ratio_of[u, k][:, h, rows] for h in range(HALVES)]
+                if k in PAIRED:
+                    parts.append(log_of[u, k][:, rows])
+                else:
+                    parts.extend(log_of[u, k][:, h, rows] for h in range(HALVES))
+                for n, part in enumerate(parts):
                     nc.tensor.matmul(
-                        out=bank[:, j, :], lhsT=source[:, h, j * P : (j + 1) * P], rhs=ident[:],
+                        out=bank[:, j, :], lhsT=part, rhs=ident[:],
                         is_transpose=True, start=(n == 0), stop=(n == len(parts) - 1),
                     )
             held["sum", u, k] = bank
@@ -362,6 +407,8 @@ def tile_deepgmm_pa_t_kernel(
         soft_exp(1)
         soft_log(0)
         softplus(0, nc.vector)
+        for k in PAIRED:
+            pair_product(0, k)
         mu_product(0)
         be_mu_rows = const.tile([P, XD], F32)
         nc.vector.tensor_copy(out=be_mu_rows[:], in_=be_mu_bf[:])
@@ -403,7 +450,8 @@ def tile_deepgmm_pa_t_kernel(
                 vector[5] = [lambda: store_mu(u + 2, 0)]
                 vector[6] = [lambda: store_mu(u + 2, 1)]
             if u + 1 < UNITS:
-                vector[4] = [lambda: softplus(u + 1, nc.gpsimd)]
+                vector.setdefault(0, []).append(lambda: softplus(u + 1, nc.gpsimd))
+                vector[3] = [lambda k=k: pair_product(u + 1, k) for k in PAIRED]
                 tensor[5] = [lambda: sig_rows(u + 1, 0)]
                 tensor[6] = [lambda: sig_rows(u + 1, 1)]
                 vector[8] = [lambda: store_sig(u + 1, 0)]
@@ -417,7 +465,7 @@ def tile_deepgmm_pa_t_kernel(
                 tensor[14] = [lambda: sig_product(u + 3, 0)]
                 tensor[15] = [lambda: sig_product(u + 3, 1)]
             if u + 1 < UNITS:
-                tensor.setdefault(15, []).append(lambda: mu_product(u + 1))
+                tensor.setdefault(14, []).append(lambda: mu_product(u + 1))
             return vector, tensor
 
         for u in range(UNITS):
@@ -431,6 +479,9 @@ def tile_deepgmm_pa_t_kernel(
             for j in range(CLUSTERS):
                 for k in range(0 if j == 0 else j + 2, min(j + 3, CLUSTERS)):
                     inverse_std(u, k)
+                if j == 0:
+                    for k in PAIRED:
+                        pair_inverse(u, k)
                 if j == CLUSTERS - 3 and u + 2 < UNITS:
                     soft_exp(u + 2)
                 for k in range(0 if j == 0 else j + 1, min(j + 2, CLUSTERS)):
@@ -439,6 +490,9 @@ def tile_deepgmm_pa_t_kernel(
                     sum_columns(u * CLUSTERS + j - SUM_LAG)
                 for stage in vector_side.get(j, []):
                     stage()
+                if j == 1:
+                    for k in PAIRED:
+                        pair_ratio(u, k)
                 square(u, j)
                 for stage in tensor_side.get(j, []):
                     stage()

@@ -26,11 +26,11 @@ UNITS = TILES // UNIT_TILES
 UNIT_ROWS = UNIT_TILES * P
 SIG_FLOOR = 1e-3
 LOG_2 = 0.6931471805599453
-LOG_BUFS = 20
-RATIO_BUFS = 13
+LOG_BUFS = 22
+RATIO_BUFS = 14
 AUX_BANKS = 3
 SUM_BANKS = 3
-PAIRED = (15,)
+PAIRED = ()
 VECTOR_SQUARES = (3, 8, 13)
 SUM_LAG = SUM_BANKS
 

@@ -32,6 +32,7 @@ AUX_BANKS = 3
 SUM_BANKS = 3
 PAIRED = ()
 VECTOR_SQUARES = (3, 8, 13)
+EARLY_TILES = (UNITS - 2) * UNIT_TILES
 SUM_LAG = SUM_BANKS
 
 ROW_PHI_MU = 0
@@ -237,6 +238,12 @@ def tile_deepgmm_pa_t_kernel(
             sp_T[u] = enc.tile([P, HALVES, UNIT_ROWS], F32, name="sp_T", bufs=2)
             engine.tensor_tensor(out=sp_T[u][:], in0=positive[u][:], in1=soft[u][:], op=ALU.add)
 
+        def first_softplus():
+            sp_T[0] = enc.tile([P, HALVES, UNIT_ROWS], F32, name="sp_T", bufs=2)
+            for h in range(HALVES):
+                nc.scalar.activation(out=soft[0][:, h, :], in_=soft[0][:, h, :], func=ACT.Ln, bias=ones_col[:])
+                nc.vector.tensor_tensor(out=sp_T[0][:, h, :], in0=positive[0][:, h, :], in1=soft[0][:, h, :], op=ALU.add)
+
         def mu_product(u):
             for h in range(HALVES):
                 acc = banks.tile([P, UNIT_ROWS], F32, tag="mu", bufs=HALVES)
@@ -405,8 +412,7 @@ def tile_deepgmm_pa_t_kernel(
         minus_abs(1, 0)
         minus_abs(1, 1)
         soft_exp(1)
-        soft_log(0)
-        softplus(0, nc.vector)
+        first_softplus()
         for k in PAIRED:
             pair_product(0, k)
         mu_product(0)
@@ -468,9 +474,43 @@ def tile_deepgmm_pa_t_kernel(
                 tensor.setdefault(14, []).append(lambda: mu_product(u + 1))
             return vector, tensor
 
+        z = const.tile([P, TILES, CLUSTERS], F32)
+        z_max = const.tile([P, TILES], F32)
+        z_exp = const.tile([P, TILES, CLUSTERS], F32)
+        z_sum = const.tile([P, TILES], F32)
+
+        def shifted_logits(a, b):
+            nc.vector.scalar_tensor_tensor(
+                out=z[:, a:b, :], in0=sums[:, a:b, :], scalar=-1.0,
+                in1=logits[:].unsqueeze(1).to_broadcast([P, b - a, CLUSTERS]), op0=ALU.mult, op1=ALU.add,
+            )
+            nc.vector.tensor_reduce(out=z_max[:, a:b], in_=z[:, a:b, :], axis=AXIS.X, op=ALU.max)
+            nc.vector.tensor_tensor(
+                out=z[:, a:b, :], in0=z[:, a:b, :],
+                in1=z_max[:, a:b].unsqueeze(2).to_broadcast([P, b - a, CLUSTERS]), op=ALU.subtract,
+            )
+
+        def logit_exp(a, b):
+            nc.scalar.activation(out=z_exp[:, a:b, :], in_=z[:, a:b, :], func=ACT.Exp)
+
+        def exp_sum(a, b):
+            nc.vector.tensor_reduce(out=z_sum[:, a:b], in_=z_exp[:, a:b, :], axis=AXIS.X, op=ALU.add)
+
+        def sum_log(a, b):
+            nc.scalar.activation(out=z_sum[:, a:b], in_=z_sum[:, a:b], func=ACT.Ln)
+
+        def store_z(a, b):
+            nc.vector.tensor_tensor(
+                out=z[:, a:b, :], in0=z[:, a:b, :],
+                in1=z_sum[:, a:b].unsqueeze(2).to_broadcast([P, b - a, CLUSTERS]), op=ALU.subtract,
+            )
+            nc.sync.dma_start(out=z_out[:, a:b, :], in_=z[:, a:b, :])
+
         for u in range(UNITS):
             for k in range(CLUSTERS):
                 log_std(u, k)
+            if u == UNITS - 1:
+                sum_log(0, EARLY_TILES)
             if u + 1 < UNITS:
                 soft_log(u + 1)
             if u == 0:
@@ -490,6 +530,14 @@ def tile_deepgmm_pa_t_kernel(
                     sum_columns(u * CLUSTERS + j - SUM_LAG)
                 for stage in vector_side.get(j, []):
                     stage()
+                if u == UNITS - 2 and j == 4:
+                    shifted_logits(0, EARLY_TILES)
+                if u == UNITS - 2 and j == 13:
+                    logit_exp(0, EARLY_TILES)
+                if u == UNITS - 2 and j == 14:
+                    exp_sum(0, EARLY_TILES)
+                if u == UNITS - 1 and j == 0:
+                    store_z(0, EARLY_TILES)
                 if j == 1:
                     for k in PAIRED:
                         pair_ratio(u, k)
@@ -500,22 +548,8 @@ def tile_deepgmm_pa_t_kernel(
         for step in range(UNITS * CLUSTERS - SUM_LAG, UNITS * CLUSTERS):
             sum_columns(step)
 
-        z = const.tile([P, TILES, CLUSTERS], F32)
-        nc.vector.scalar_tensor_tensor(
-            out=z[:], in0=sums[:], scalar=-1.0, in1=logits[:].unsqueeze(1).to_broadcast([P, TILES, CLUSTERS]),
-            op0=ALU.mult, op1=ALU.add,
-        )
-        z_max = const.tile([P, TILES], F32)
-        nc.vector.tensor_reduce(out=z_max[:], in_=z[:], axis=AXIS.X, op=ALU.max)
-        nc.vector.tensor_tensor(
-            out=z[:], in0=z[:], in1=z_max[:].unsqueeze(2).to_broadcast([P, TILES, CLUSTERS]), op=ALU.subtract
-        )
-        z_exp = const.tile([P, TILES, CLUSTERS], F32)
-        nc.scalar.activation(out=z_exp[:], in_=z[:], func=ACT.Exp)
-        z_sum = const.tile([P, TILES], F32)
-        nc.vector.tensor_reduce(out=z_sum[:], in_=z_exp[:], axis=AXIS.X, op=ALU.add)
-        nc.scalar.activation(out=z_sum[:], in_=z_sum[:], func=ACT.Ln)
-        nc.vector.tensor_tensor(
-            out=z[:], in0=z[:], in1=z_sum[:].unsqueeze(2).to_broadcast([P, TILES, CLUSTERS]), op=ALU.subtract
-        )
-        nc.sync.dma_start(out=z_out, in_=z[:])
+        shifted_logits(EARLY_TILES, TILES)
+        logit_exp(EARLY_TILES, TILES)
+        exp_sum(EARLY_TILES, TILES)
+        sum_log(EARLY_TILES, TILES)
+        store_z(EARLY_TILES, TILES)

@@ -26,12 +26,12 @@ UNITS = TILES // UNIT_TILES
 UNIT_ROWS = UNIT_TILES * P
 SIG_FLOOR = 1e-3
 LOG_2 = 0.6931471805599453
-LOG_BUFS = 22
-RATIO_BUFS = 14
+LOG_BUFS = 20
+RATIO_BUFS = 13
 AUX_BANKS = 3
 SUM_BANKS = 3
-PAIRED = ()
-VECTOR_SQUARES = (3, 8, 13)
+PAIRED = (15,)
+VECTOR_SQUARES = (0, 1, 4, 8, 12)
 EARLY_TILES = (UNITS - 2) * UNIT_TILES
 SUM_LAG = SUM_BANKS
 

@@ -31,7 +31,7 @@ RATIO_BUFS = 13
 AUX_BANKS = 3
 SUM_BANKS = 3
 PAIRED = (15,)
-VECTOR_SQUARES = (0, 1, 4, 8, 12)
+VECTOR_SQUARES = (0, 1, 6, 11)
 EARLY_TILES = (UNITS - 2) * UNIT_TILES
 SUM_LAG = SUM_BANKS
 

@@ -25,13 +25,14 @@ UNIT_PAIRS = UNIT_TILES // 2
 UNITS = TILES // UNIT_TILES
 UNIT_ROWS = UNIT_TILES * P
 SIG_FLOOR = 1e-3
+SOFT_CAP = 60.0
 LOG_2 = 0.6931471805599453
 LOG_BUFS = 20
 RATIO_BUFS = 13
 AUX_BANKS = 3
 SUM_BANKS = 3
 PAIRED = (15,)
-VECTOR_SQUARES = (0, 1, 6, 11)
+VECTOR_SQUARES = (1, 6, 11)
 EARLY_TILES = (UNITS - 2) * UNIT_TILES
 SUM_LAG = SUM_BANKS
 
@@ -154,7 +155,6 @@ def tile_deepgmm_pa_t_kernel(
         grouped = {}
         codes = {}
         planes = {}
-        positive = {}
         soft = {}
         sp_T = {}
         mu_ps = {}
@@ -202,47 +202,32 @@ def tile_deepgmm_pa_t_kernel(
             product(acc, 1, h, u)
             held["sig", u, h] = acc
 
-        def positive_part(u, h):
-            if h == 0:
-                positive[u] = enc.tile([P, HALVES, UNIT_ROWS], F32, name="positive", bufs=2)
-            if u < 2:
-                nc.scalar.activation(
-                    out=positive[u][:, h, :], in_=held["sig", u, h][:], func=ACT.Relu,
-                    bias=params[:, h, ROW_BE_SIG : ROW_BE_SIG + 1],
-                )
-            else:
-                nc.vector.tensor_scalar(
-                    out=positive[u][:, h, :], in0=held["sig", u, h][:],
-                    scalar1=params[:, h, ROW_BE_SIG : ROW_BE_SIG + 1], scalar2=0.0, op0=ALU.add, op1=ALU.max,
-                )
-
-        def minus_abs(u, h):
+        def capped(u, h):
             if h == 0:
                 soft[u] = enc.tile([P, HALVES, UNIT_ROWS], F32, name="soft", bufs=2)
-            nc.vector.scalar_tensor_tensor(
-                out=soft[u][:, h, :], in0=positive[u][:, h, :], scalar=-2.0, in1=held["sig", u, h][:],
-                op0=ALU.mult, op1=ALU.add,
+            nc.vector.tensor_scalar(
+                out=soft[u][:, h, :], in0=held["sig", u, h][:],
+                scalar1=params[:, h, ROW_BE_SIG : ROW_BE_SIG + 1], scalar2=SOFT_CAP, op0=ALU.add, op1=ALU.min,
             )
 
         def soft_exp(u):
-            for h in range(HALVES):
-                nc.scalar.activation(
-                    out=soft[u][:, h, :], in_=soft[u][:, h, :], func=ACT.Exp,
-                    bias=params[:, h, ROW_BE_SIG : ROW_BE_SIG + 1],
-                )
+            nc.scalar.activation(out=soft[u][:], in_=soft[u][:], func=ACT.Exp)
 
         def soft_log(u):
             nc.scalar.activation(out=soft[u][:], in_=soft[u][:], func=ACT.Ln, bias=ones_col[:])
 
-        def softplus(u, engine):
-            sp_T[u] = enc.tile([P, HALVES, UNIT_ROWS], F32, name="sp_T", bufs=2)
-            engine.tensor_tensor(out=sp_T[u][:], in0=positive[u][:], in1=soft[u][:], op=ALU.add)
+        def softplus(u, h):
+            if h == 0:
+                sp_T[u] = enc.tile([P, HALVES, UNIT_ROWS], F32, name="sp_T", bufs=2)
+            nc.vector.scalar_tensor_tensor(
+                out=sp_T[u][:, h, :], in0=held["sig", u, h][:], scalar=params[:, h, ROW_BE_SIG : ROW_BE_SIG + 1],
+                in1=soft[u][:, h, :], op0=ALU.add, op1=ALU.max,
+            )
 
         def first_softplus():
-            sp_T[0] = enc.tile([P, HALVES, UNIT_ROWS], F32, name="sp_T", bufs=2)
             for h in range(HALVES):
                 nc.scalar.activation(out=soft[0][:, h, :], in_=soft[0][:, h, :], func=ACT.Ln, bias=ones_col[:])
-                nc.vector.tensor_tensor(out=sp_T[0][:, h, :], in0=positive[0][:, h, :], in1=soft[0][:, h, :], op=ALU.add)
+                softplus(0, h)
 
         def mu_product(u):
             for h in range(HALVES):
@@ -399,19 +384,17 @@ def tile_deepgmm_pa_t_kernel(
         group_y(1, 0)
         group_y(1, 1)
         sig_product(0, 1)
-        positive_part(0, 0)
-        positive_part(0, 1)
-        minus_abs(0, 0)
-        minus_abs(0, 1)
+        capped(0, 0)
+        capped(0, 1)
         soft_exp(0)
         quantise(1)
         sig_product(1, 0)
         sig_product(1, 1)
-        positive_part(1, 0)
-        positive_part(1, 1)
-        minus_abs(1, 0)
-        minus_abs(1, 1)
+        capped(1, 0)
+        capped(1, 1)
         soft_exp(1)
+        sig_product(0, 0)
+        sig_product(0, 1)
         first_softplus()
         for k in PAIRED:
             pair_product(0, k)
@@ -448,26 +431,28 @@ def tile_deepgmm_pa_t_kernel(
             if u + 4 < UNITS:
                 vector[0] = [lambda: load_y(u + 4)]
             if u + 2 < UNITS:
-                vector.setdefault(0, []).append(lambda: positive_part(u + 2, 0))
-                vector[1] = [lambda: positive_part(u + 2, 1)]
-                vector[2] = [lambda: minus_abs(u + 2, 0), lambda: minus_abs(u + 2, 1)]
+                vector.setdefault(0, []).append(lambda: capped(u + 2, 0))
+                vector[1] = [lambda: capped(u + 2, 1)]
                 tensor[2] = [lambda: mu_rows(u + 2, 0)]
                 tensor[3] = [lambda: mu_rows(u + 2, 1)]
                 vector[5] = [lambda: store_mu(u + 2, 0)]
                 vector[6] = [lambda: store_mu(u + 2, 1)]
             if u + 1 < UNITS:
-                vector.setdefault(0, []).append(lambda: softplus(u + 1, nc.gpsimd))
-                vector[3] = [lambda k=k: pair_product(u + 1, k) for k in PAIRED]
-                tensor[5] = [lambda: sig_rows(u + 1, 0)]
-                tensor[6] = [lambda: sig_rows(u + 1, 1)]
-                vector[8] = [lambda: store_sig(u + 1, 0)]
-                vector[9] = [lambda: store_sig(u + 1, 1)]
+                tensor[0] = [lambda: sig_product(u + 1, 0)]
+                tensor[1] = [lambda: sig_product(u + 1, 1)]
+                vector[3] = [lambda: softplus(u + 1, 0)]
+                vector[4] = [lambda: softplus(u + 1, 1)]
+                vector.setdefault(5, []).extend([lambda k=k: pair_product(u + 1, k) for k in PAIRED])
+                tensor[6] = [lambda: sig_rows(u + 1, 0)]
+                tensor[7] = [lambda: sig_rows(u + 1, 1)]
+                vector[9] = [lambda: store_sig(u + 1, 0)]
+                vector[10] = [lambda: store_sig(u + 1, 1)]
             if u + 3 < UNITS:
-                tensor[8] = [lambda: turn_y(u + 3, 0)]
-                tensor[9] = [lambda: turn_y(u + 3, 1)]
-                vector[11] = [lambda: group_y(u + 3, 0)]
-                vector[12] = [lambda: group_y(u + 3, 1)]
-                vector[13] = [lambda: quantise(u + 3)]
+                tensor[9] = [lambda: turn_y(u + 3, 0)]
+                tensor[10] = [lambda: turn_y(u + 3, 1)]
+                vector[12] = [lambda: group_y(u + 3, 0)]
+                vector[13] = [lambda: group_y(u + 3, 1)]
+                vector[14] = [lambda: quantise(u + 3)]
                 tensor[14] = [lambda: sig_product(u + 3, 0)]
                 tensor[15] = [lambda: sig_product(u + 3, 1)]
             if u + 1 < UNITS:

@@ -31,7 +31,7 @@ LOG_BUFS = 20
 RATIO_BUFS = 13
 AUX_BANKS = 3
 SUM_BANKS = 3
-PAIRED = (15,)
+PAIR_BUFS = 4
 VECTOR_SQUARES = (1, 6, 11)
 EARLY_TILES = (UNITS - 2) * UNIT_TILES
 SUM_LAG = SUM_BANKS
@@ -42,6 +42,10 @@ ROW_BE_MU = 2 * CLUSTERS
 ROW_BE_SIG = 2 * CLUSTERS + 1
 
 FLOPS = 2 * ROWS * YD * 2 * XD
+
+
+def paired(u):
+    return (14, 15) if u == 0 else (15,)
 
 
 def tile_deepgmm_pa_t_kernel(
@@ -114,7 +118,10 @@ def tile_deepgmm_pa_t_kernel(
                     in_=scales[0, 4 * quadrant : 4 * quadrant + 4, :].bitcast(I32),
                 )
 
-        load_y(0)
+        first_rows = enc.tile([P, UNIT_TILES, YD], BF16, name="y_rows", bufs=4)
+        for pair in range(UNIT_PAIRS):
+            nc.sync.dma_start(out=first_rows[:, 2 * pair : 2 * pair + 2, :], in_=y_tiles[:, 2 * pair : 2 * pair + 2, :])
+        y_loaded[0] = first_rows
         nc.sync.dma_start(out=param_rows_bf[ROW_PHI_MU : ROW_PHI_MU + CLUSTERS, :], in_=phi_mus)
         nc.sync.dma_start(out=param_rows_bf[ROW_PHI_SIG : ROW_PHI_SIG + CLUSTERS, :], in_=phi_sigs)
         nc.sync.dma_start(out=param_rows_bf[ROW_BE_MU : ROW_BE_MU + 1, :], in_=be_mu.unsqueeze(0))
@@ -172,11 +179,11 @@ def tile_deepgmm_pa_t_kernel(
                     )
             held["y", u, pair] = y_T
 
-        def group_y(u, pair):
+        def group_y(u, pair, copy=None):
             if pair == 0:
                 grouped[u] = enc.tile([P, UNIT_ROWS * 4], BF16, name="grouped", bufs=2, align_bytes=64)
             grouped_words = grouped[u][:].bitcast(F32).rearrange("p (n w) -> p n w", w=2)
-            nc.vector.tensor_copy(
+            (copy or nc.vector.tensor_copy)(
                 out=grouped_words[:, 2 * pair * P : (2 * pair + 2) * P, :],
                 in_=held["y", u, pair][:].rearrange("p w n -> p n w"),
             )
@@ -212,6 +219,9 @@ def tile_deepgmm_pa_t_kernel(
 
         def soft_exp(u):
             nc.scalar.activation(out=soft[u][:], in_=soft[u][:], func=ACT.Exp)
+
+        def half_exp(u, h):
+            nc.scalar.activation(out=soft[u][:, h, :], in_=soft[u][:, h, :], func=ACT.Exp)
 
         def soft_log(u):
             nc.scalar.activation(out=soft[u][:], in_=soft[u][:], func=ACT.Ln, bias=ones_col[:])
@@ -289,19 +299,19 @@ def tile_deepgmm_pa_t_kernel(
             return "vector" if k in VECTOR_SQUARES else "gpsimd"
 
         def pair_product(u, k):
-            swapped = ratios.tile([P, HALVES, UNIT_ROWS], F32, name="swapped", bufs=2 * len(PAIRED))
+            swapped = ratios.tile([P, HALVES, UNIT_ROWS], F32, name="swapped", bufs=PAIR_BUFS)
             for h in range(HALVES):
                 nc.gpsimd.tensor_scalar(
                     out=swapped[:, h, :], in0=sp_T[u][:, 1 - h, :],
                     scalar1=spread[:, 1 - h, k : k + 1], scalar2=1.0, op0=ALU.add, op1=ALU.mult,
                 )
-            pair_log = logs.tile([P, UNIT_ROWS], F32, name="pair_log", bufs=2 * len(PAIRED))
+            pair_log = logs.tile([P, UNIT_ROWS], F32, name="pair_log", bufs=PAIR_BUFS)
             nc.gpsimd.tensor_tensor(out=pair_log[:], in0=swapped[:, 0, :], in1=swapped[:, 1, :], op=ALU.mult)
             ratio_of[u, k] = swapped
             log_of[u, k] = pair_log
 
         def pair_inverse(u, k):
-            inverse = ratios.tile([P, UNIT_ROWS], F32, name="inverse", bufs=2 * len(PAIRED))
+            inverse = ratios.tile([P, UNIT_ROWS], F32, name="inverse", bufs=PAIR_BUFS)
             nc.scalar.activation(out=inverse[:], in_=log_of[u, k][:], func=ACT.Exp, scale=-1.0, bias=half_col[:])
             held["inverse", u, k] = inverse
 
@@ -312,7 +322,7 @@ def tile_deepgmm_pa_t_kernel(
             )
 
         def log_std(u, k):
-            if k in PAIRED:
+            if k in paired(u):
                 nc.scalar.activation(out=log_of[u, k][:], in_=log_of[u, k][:], func=ACT.Ln)
                 return
             log_t = logs.tile([P, HALVES, UNIT_ROWS], F32, name="log_t")
@@ -323,7 +333,7 @@ def tile_deepgmm_pa_t_kernel(
             log_of[u, k] = log_t
 
         def inverse_std(u, k):
-            if k in PAIRED:
+            if k in paired(u):
                 return
             ratio = ratios.tile([P, HALVES, UNIT_ROWS], F32, name="ratio")
             if squarer(u, k) == "vector":
@@ -353,7 +363,7 @@ def tile_deepgmm_pa_t_kernel(
             for j in range(UNIT_TILES):
                 rows = slice(j * P, (j + 1) * P)
                 parts = [ratio_of[u, k][:, h, rows] for h in range(HALVES)]
-                if k in PAIRED:
+                if k in paired(u):
                     parts.append(log_of[u, k][:, rows])
                 else:
                     parts.extend(log_of[u, k][:, h, rows] for h in range(HALVES))
@@ -376,27 +386,29 @@ def tile_deepgmm_pa_t_kernel(
         turn_params()
         group_y(0, 0)
         group_y(0, 1)
-        derive_params()
         quantise(0)
+        derive_params()
         turn_y(1, 0)
         turn_y(1, 1)
         sig_product(0, 0)
-        group_y(1, 0)
-        group_y(1, 1)
+        group_y(1, 0, nc.scalar.copy)
+        group_y(1, 1, nc.scalar.copy)
         sig_product(0, 1)
         capped(0, 0)
-        capped(0, 1)
-        soft_exp(0)
+        half_exp(0, 0)
         quantise(1)
+        capped(0, 1)
+        half_exp(0, 1)
         sig_product(1, 0)
         sig_product(1, 1)
         capped(1, 0)
+        half_exp(1, 0)
         capped(1, 1)
-        soft_exp(1)
+        half_exp(1, 1)
         sig_product(0, 0)
         sig_product(0, 1)
         first_softplus()
-        for k in PAIRED:
+        for k in paired(0):
             pair_product(0, k)
         mu_product(0)
         be_mu_rows = const.tile([P, XD], F32)
@@ -442,7 +454,7 @@ def tile_deepgmm_pa_t_kernel(
                 tensor[1] = [lambda: sig_product(u + 1, 1)]
                 vector[3] = [lambda: softplus(u + 1, 0)]
                 vector[4] = [lambda: softplus(u + 1, 1)]
-                vector.setdefault(5, []).extend([lambda k=k: pair_product(u + 1, k) for k in PAIRED])
+                vector.setdefault(5, []).extend([lambda k=k: pair_product(u + 1, k) for k in paired(u + 1)])
                 tensor[6] = [lambda: sig_rows(u + 1, 0)]
                 tensor[7] = [lambda: sig_rows(u + 1, 1)]
                 vector[9] = [lambda: store_sig(u + 1, 0)]
@@ -505,7 +517,7 @@ def tile_deepgmm_pa_t_kernel(
                 for k in range(0 if j == 0 else j + 2, min(j + 3, CLUSTERS)):
                     inverse_std(u, k)
                 if j == 0:
-                    for k in PAIRED:
+                    for k in paired(u):
                         pair_inverse(u, k)
                 if j == CLUSTERS - 3 and u + 2 < UNITS:
                     soft_exp(u + 2)
@@ -524,7 +536,7 @@ def tile_deepgmm_pa_t_kernel(
                 if u == UNITS - 1 and j == 0:
                     store_z(0, EARLY_TILES)
                 if j == 1:
-                    for k in PAIRED:
+                    for k in paired(u):
                         pair_ratio(u, k)
                 square(u, j)
                 for stage in tensor_side.get(j, []):

@@ -32,7 +32,6 @@ RATIO_BUFS = 13
 AUX_BANKS = 3
 SUM_BANKS = 3
 PAIR_BUFS = 4
-VECTOR_SQUARES = (1, 6, 11)
 EARLY_TILES = (UNITS - 2) * UNIT_TILES
 SUM_LAG = SUM_BANKS
 
@@ -45,7 +44,11 @@ FLOPS = 2 * ROWS * YD * 2 * XD
 
 
 def paired(u):
-    return (14, 15) if u == 0 else (15,)
+    return (13, 14, 15) if u == 0 else (15,)
+
+
+def vector_squares(u):
+    return (1, 2, 3, 7, 11) if u == 0 else (1, 6, 11)
 
 
 def tile_deepgmm_pa_t_kernel(
@@ -295,8 +298,8 @@ def tile_deepgmm_pa_t_kernel(
 
         def squarer(u, k):
             if u == UNITS - 1:
-                return "scalar" if k % 2 == 1 else "gpsimd"
-            return "vector" if k in VECTOR_SQUARES else "gpsimd"
+                return "scalar" if k % 2 == 1 or k == CLUSTERS - 2 else "gpsimd"
+            return "vector" if k in vector_squares(u) else "gpsimd"
 
         def pair_product(u, k):
             swapped = ratios.tile([P, HALVES, UNIT_ROWS], F32, name="swapped", bufs=PAIR_BUFS)

@@ -31,7 +31,7 @@ LOG_BUFS = 20
 RATIO_BUFS = 13
 AUX_BANKS = 3
 SUM_BANKS = 3
-PAIR_BUFS = 4
+PAIR_BUFS = 5
 EARLY_TILES = (UNITS - 2) * UNIT_TILES
 SUM_LAG = SUM_BANKS
 
@@ -44,11 +44,11 @@ FLOPS = 2 * ROWS * YD * 2 * XD
 
 
 def paired(u):
-    return (13, 14, 15) if u == 0 else (15,)
+    return (12, 13, 14, 15) if u == 0 else (15,)
 
 
 def vector_squares(u):
-    return (1, 2, 3, 7, 11) if u == 0 else (1, 6, 11)
+    return (1, 2, 3, 4, 7, 10) if u == 0 else (1, 5, 10)
 
 
 def tile_deepgmm_pa_t_kernel(
@@ -184,7 +184,7 @@ def tile_deepgmm_pa_t_kernel(
 
         def group_y(u, pair, copy=None):
             if pair == 0:
-                grouped[u] = enc.tile([P, UNIT_ROWS * 4], BF16, name="grouped", bufs=2, align_bytes=64)
+                grouped[u] = enc.tile([P, UNIT_ROWS * 4], BF16, name="grouped", bufs=1, align_bytes=64)
             grouped_words = grouped[u][:].bitcast(F32).rearrange("p (n w) -> p n w", w=2)
             (copy or nc.vector.tensor_copy)(
                 out=grouped_words[:, 2 * pair * P : (2 * pair + 2) * P, :],
@@ -192,8 +192,8 @@ def tile_deepgmm_pa_t_kernel(
             )
 
         def quantise(u):
-            codes[u] = enc.tile([P, UNIT_ROWS], U32, name="y_codes", bufs=4, align_bytes=64)
-            planes[u] = enc.tile([P, UNIT_ROWS], U8, name="y_planes", bufs=4, align_bytes=64)
+            codes[u] = enc.tile([P, UNIT_ROWS], U32, name="y_codes", bufs=3, align_bytes=64)
+            planes[u] = enc.tile([P, UNIT_ROWS], U8, name="y_planes", bufs=3, align_bytes=64)
             nc.vector.quantize_mx(out=codes[u][:].bitcast(FP8X4), scales=planes[u][:], in_=grouped[u][:])
 
         def product(acc, w, h, u):
@@ -268,7 +268,7 @@ def tile_deepgmm_pa_t_kernel(
             held["mu", u, pair] = bank
 
         def store_mu(u, pair):
-            out_rows = enc.tile([P, 2, XD], F32, name="out_rows", bufs=4)
+            out_rows = enc.tile([P, 2, XD], F32, name="out_rows", bufs=3)
             nc.vector.tensor_tensor(
                 out=out_rows[:], in0=held["mu", u, pair][:],
                 in1=be_mu_rows[:].unsqueeze(1).to_broadcast([P, 2, XD]), op=ALU.add,
@@ -286,7 +286,7 @@ def tile_deepgmm_pa_t_kernel(
             held["sp", u, pair] = bank
 
         def store_sig(u, pair):
-            out_rows = enc.tile([P, 2, XD], F32, name="out_rows", bufs=4)
+            out_rows = enc.tile([P, 2, XD], F32, name="out_rows", bufs=3)
             nc.vector.tensor_scalar(
                 out=out_rows[:], in0=held["sp", u, pair][:], scalar1=SIG_FLOOR, scalar2=None, op0=ALU.add
             )

@@ -28,10 +28,10 @@ SIG_FLOOR = 1e-3
 SOFT_CAP = 60.0
 LOG_2 = 0.6931471805599453
 LOG_BUFS = 20
-RATIO_BUFS = 13
+RATIO_BUFS = 12
 AUX_BANKS = 3
 SUM_BANKS = 3
-PAIR_BUFS = 5
+PAIR_BUFS = 6
 EARLY_TILES = (UNITS - 2) * UNIT_TILES
 SUM_LAG = SUM_BANKS
 
@@ -44,7 +44,7 @@ FLOPS = 2 * ROWS * YD * 2 * XD
 
 
 def paired(u):
-    return (12, 13, 14, 15) if u == 0 else (15,)
+    return (11, 12, 13, 14, 15) if u == 0 else (15,)
 
 
 def vector_squares(u):
@@ -303,13 +303,14 @@ def tile_deepgmm_pa_t_kernel(
 
         def pair_product(u, k):
             swapped = ratios.tile([P, HALVES, UNIT_ROWS], F32, name="swapped", bufs=PAIR_BUFS)
+            eng = nc.vector if (u == 0 and k in (11, 12)) else nc.gpsimd
             for h in range(HALVES):
-                nc.gpsimd.tensor_scalar(
+                eng.tensor_scalar(
                     out=swapped[:, h, :], in0=sp_T[u][:, 1 - h, :],
                     scalar1=spread[:, 1 - h, k : k + 1], scalar2=1.0, op0=ALU.add, op1=ALU.mult,
                 )
             pair_log = logs.tile([P, UNIT_ROWS], F32, name="pair_log", bufs=PAIR_BUFS)
-            nc.gpsimd.tensor_tensor(out=pair_log[:], in0=swapped[:, 0, :], in1=swapped[:, 1, :], op=ALU.mult)
+            eng.tensor_tensor(out=pair_log[:], in0=swapped[:, 0, :], in1=swapped[:, 1, :], op=ALU.mult)
             ratio_of[u, k] = swapped
             log_of[u, k] = pair_log
 
@@ -319,7 +320,7 @@ def tile_deepgmm_pa_t_kernel(
             held["inverse", u, k] = inverse
 
         def pair_ratio(u, k):
-            nc.gpsimd.tensor_tensor(
+            (nc.vector if (u == 0 and k in (11,)) else nc.gpsimd).tensor_tensor(
                 out=ratio_of[u, k][:], in0=ratio_of[u, k][:],
                 in1=held["inverse", u, k][:].unsqueeze(1).to_broadcast([P, HALVES, UNIT_ROWS]), op=ALU.mult,
             )
@@ -439,13 +440,19 @@ def tile_deepgmm_pa_t_kernel(
             store_sig(0, 0)
             store_sig(0, 1)
             sig_product(2, 1)
+            capped(2, 0)
+            capped(2, 1)
+            mu_rows(2, 0)
+            mu_rows(2, 1)
+            store_mu(2, 0)
+            store_mu(2, 1)
 
         def side_work(u):
             vector = {}
             tensor = {}
             if u + 4 < UNITS:
                 vector[0] = [lambda: load_y(u + 4)]
-            if u + 2 < UNITS:
+            if 0 < u and u + 2 < UNITS:
                 vector.setdefault(0, []).append(lambda: capped(u + 2, 0))
                 vector[1] = [lambda: capped(u + 2, 1)]
                 tensor[2] = [lambda: mu_rows(u + 2, 0)]
@@ -476,7 +483,6 @@ def tile_deepgmm_pa_t_kernel(
 
         z = const.tile([P, TILES, CLUSTERS], F32)
         z_max = const.tile([P, TILES], F32)
-        z_exp = const.tile([P, TILES, CLUSTERS], F32)
         z_sum = const.tile([P, TILES], F32)
 
         def shifted_logits(a, b):
@@ -491,10 +497,10 @@ def tile_deepgmm_pa_t_kernel(
             )
 
         def logit_exp(a, b):
-            nc.scalar.activation(out=z_exp[:, a:b, :], in_=z[:, a:b, :], func=ACT.Exp)
+            nc.scalar.activation(out=sums[:, a:b, :], in_=z[:, a:b, :], func=ACT.Exp)
 
         def exp_sum(a, b):
-            nc.vector.tensor_reduce(out=z_sum[:, a:b], in_=z_exp[:, a:b, :], axis=AXIS.X, op=ALU.add)
+            nc.vector.tensor_reduce(out=z_sum[:, a:b], in_=sums[:, a:b, :], axis=AXIS.X, op=ALU.add)
 
         def sum_log(a, b):
             nc.scalar.activation(out=z_sum[:, a:b], in_=z_sum[:, a:b], func=ACT.Ln)

from contextlib import ExitStack

import concourse.masks as masks
import concourse.mybir as mybir

F32 = mybir.dt.float32
BF16 = mybir.dt.bfloat16
I32 = mybir.dt.int32
U32 = mybir.dt.uint32
U8 = mybir.dt.uint8
FP8X4 = mybir.dt.float8_e4m3fn_x4
ACT = mybir.ActivationFunctionType
ALU = mybir.AluOpType
AXIS = mybir.AxisListType

P = 128
ROWS = 4096
YD = 512
XD = 256
HALVES = XD // P
CLUSTERS = 16
TILES = ROWS // P
UNIT_TILES = 4
UNIT_PAIRS = UNIT_TILES // 2
UNITS = TILES // UNIT_TILES
UNIT_ROWS = UNIT_TILES * P
SIG_FLOOR = 1e-3
SOFT_CAP = 60.0
LOG_2 = 0.6931471805599453
LOG_BUFS = 20
RATIO_BUFS = 12
AUX_BANKS = 3
SUM_BANKS = 3
PAIR_BUFS = 6
EARLY_TILES = (UNITS - 2) * UNIT_TILES
SUM_LAG = SUM_BANKS

ROW_PHI_MU = 0
ROW_PHI_SIG = CLUSTERS
ROW_BE_MU = 2 * CLUSTERS
ROW_BE_SIG = 2 * CLUSTERS + 1

FLOPS = 2 * ROWS * YD * 2 * XD


def paired(u):
    return (11, 12, 13, 14, 15) if u == 0 else (15,)


def vector_squares(u):
    return (1, 2, 3, 4, 7, 10) if u == 0 else (1, 5, 10)


def tile_deepgmm_pa_t_kernel(
    tc,
    Y,
    We_mu_words,
    We_mu_scales,
    be_mu,
    We_sig_words,
    We_sig_scales,
    be_sig,
    phi_mus,
    phi_sigs,
    phi_logits,
    out_0,
    out_1,
    out_2,
):
    nc = tc.nc
    y_tiles = Y.rearrange("(p i) k -> p i k", i=TILES)
    mu_out = out_0.rearrange("(p i) d -> p i d", i=TILES)
    sig_out = out_1.rearrange("(p i) d -> p i d", i=TILES)
    z_out = out_2.rearrange("(p i) k -> p i k", i=TILES)

    with ExitStack() as ctx:
        ctx.enter_context(tc.manual_schedule())
        const = ctx.enter_context(tc.tile_pool(name="const", bufs=1))
        enc = ctx.enter_context(tc.tile_pool(name="enc", bufs=2))
        logs = ctx.enter_context(tc.tile_pool(name="logs", bufs=LOG_BUFS))
        ratios = ctx.enter_context(tc.tile_pool(name="ratios", bufs=RATIO_BUFS))
        banks = ctx.enter_context(tc.psum_pool(name="banks", bufs=AUX_BANKS))

        ident = const.tile([P, P], F32)
        masks.make_identity(nc, ident[:])
        w_words = const.tile([P, 2, XD], U32, align_bytes=64)
        w_planes = const.tile([P, 2, XD], U8, align_bytes=64)
        nc.vector.memset(w_planes[:].rearrange("p w n -> p (w n)").bitcast(I32), 0)
        param_rows_bf = const.tile([P, XD], BF16)
        nc.vector.memset(param_rows_bf[:].bitcast(I32), 0)
        zero_col = const.tile([P, 1], F32)
        nc.vector.memset(zero_col[:], 0.0)
        ones_col = const.tile([P, 1], F32)
        nc.vector.memset(ones_col[:], 1.0)
        half_col = const.tile([P, 1], F32)
        nc.vector.tensor_scalar(
            out=half_col[:], in0=zero_col[:], scalar1=-0.5 * LOG_2, scalar2=None, op0=ALU.add
        )
        full_col = const.tile([P, 1], F32)
        nc.vector.tensor_scalar(out=full_col[:], in0=zero_col[:], scalar1=-LOG_2, scalar2=None, op0=ALU.add)
        warm_col = const.tile([P, 1], F32)
        nc.scalar.activation(out=warm_col[:], in_=zero_col[:], func=ACT.Exp)
        logits_bf = const.tile([P, CLUSTERS], BF16)
        be_mu_bf = const.tile([P, XD], BF16)

        y_loaded = {}

        def load_y(u):
            y_rows = enc.tile([P, UNIT_TILES, YD], BF16, name="y_rows", bufs=4)
            nc.sync.dma_start(out=y_rows[:], in_=y_tiles[:, u * UNIT_TILES : (u + 1) * UNIT_TILES, :])
            y_loaded[u] = y_rows

        def load_weight(w, words, scales):
            nc.sync.dma_start(
                out=w_words[:, w, :].bitcast(I32),
                in_=words[0].rearrange("p n t -> p (n t)").bitcast(I32),
            )
            for quadrant in range(4):
                nc.sync.dma_start(
                    out=w_planes[32 * quadrant : 32 * quadrant + 4, w, :].bitcast(I32),
                    in_=scales[0, 4 * quadrant : 4 * quadrant + 4, :].bitcast(I32),
                )

        first_rows = enc.tile([P, UNIT_TILES, YD], BF16, name="y_rows", bufs=4)
        for pair in range(UNIT_PAIRS):
            nc.sync.dma_start(out=first_rows[:, 2 * pair : 2 * pair + 2, :], in_=y_tiles[:, 2 * pair : 2 * pair + 2, :])
        y_loaded[0] = first_rows
        nc.sync.dma_start(out=param_rows_bf[ROW_PHI_MU : ROW_PHI_MU + CLUSTERS, :], in_=phi_mus)
        nc.sync.dma_start(out=param_rows_bf[ROW_PHI_SIG : ROW_PHI_SIG + CLUSTERS, :], in_=phi_sigs)
        nc.sync.dma_start(out=param_rows_bf[ROW_BE_MU : ROW_BE_MU + 1, :], in_=be_mu.unsqueeze(0))
        nc.sync.dma_start(out=param_rows_bf[ROW_BE_SIG : ROW_BE_SIG + 1, :], in_=be_sig.unsqueeze(0))
        load_weight(1, We_sig_words, We_sig_scales)
        load_y(1)
        load_weight(0, We_mu_words, We_mu_scales)
        load_y(2)
        load_y(3)
        nc.sync.dma_start(out=be_mu_bf[:], in_=be_mu.partition_broadcast(P))
        nc.sync.dma_start(out=logits_bf[:], in_=phi_logits.partition_broadcast(P))

        params = const.tile([P, HALVES, P], F32)
        shift = const.tile([P, HALVES, CLUSTERS], F32)
        spread = const.tile([P, HALVES, CLUSTERS], F32)
        held = {}

        def turn_params():
            param_rows = const.tile([P, XD], F32)
            nc.vector.tensor_copy(out=param_rows[:], in_=param_rows_bf[:])
            params_ps = banks.tile([P, HALVES, P], F32, tag="aux", bufs=AUX_BANKS)
            for h in range(HALVES):
                nc.tensor.transpose(out=params_ps[:, h, :], in_=param_rows[:, h * P : (h + 1) * P], identity=ident[:])
            held["params"] = params_ps

        def derive_params():
            nc.vector.tensor_copy(out=params[:], in_=held["params"][:])
            for h in range(HALVES):
                nc.vector.tensor_scalar(
                    out=shift[:, h, :], in0=params[:, h, ROW_PHI_MU : ROW_PHI_MU + CLUSTERS],
                    scalar1=params[:, h, ROW_BE_MU : ROW_BE_MU + 1], scalar2=None, op0=ALU.subtract,
                )
            nc.vector.tensor_scalar(
                out=spread[:], in0=params[:, :, ROW_PHI_SIG : ROW_PHI_SIG + CLUSTERS],
                scalar1=SIG_FLOOR, scalar2=None, op0=ALU.add,
            )

        grouped = {}
        codes = {}
        planes = {}
        soft = {}
        sp_T = {}
        mu_ps = {}

        def turn_y(u, pair):
            y_words = y_loaded[u][:].rearrange("p j k -> p (j k)").bitcast(F32)
            y_T = banks.tile([P, 2, 2 * P], F32, tag="aux", bufs=AUX_BANKS)
            for two in range(2):
                first_word = (2 * pair + two) * (YD // 2)
                for w in range(2):
                    nc.tensor.transpose(
                        out=y_T[:, w, two * P : (two + 1) * P],
                        in_=y_words[:, first_word + w : first_word + YD // 2 : 2],
                        identity=ident[:],
                    )
            held["y", u, pair] = y_T

        def group_y(u, pair, copy=None):
            if pair == 0:
                grouped[u] = enc.tile([P, UNIT_ROWS * 4], BF16, name="grouped", bufs=1, align_bytes=64)
            grouped_words = grouped[u][:].bitcast(F32).rearrange("p (n w) -> p n w", w=2)
            (copy or nc.vector.tensor_copy)(
                out=grouped_words[:, 2 * pair * P : (2 * pair + 2) * P, :],
                in_=held["y", u, pair][:].rearrange("p w n -> p n w"),
            )

        def quantise(u):
            codes[u] = enc.tile([P, UNIT_ROWS], U32, name="y_codes", bufs=3, align_bytes=64)
            planes[u] = enc.tile([P, UNIT_ROWS], U8, name="y_planes", bufs=3, align_bytes=64)
            nc.vector.quantize_mx(out=codes[u][:].bitcast(FP8X4), scales=planes[u][:], in_=grouped[u][:])

        def product(acc, w, h, u):
            nc.tensor.matmul_mx(
                out=acc[:],
                lhsT=w_words[:, w, h * P : (h + 1) * P].bitcast(FP8X4),
                lhsT_scale=w_planes[:, w, h * P : (h + 1) * P],
                rhs=codes[u][:].bitcast(FP8X4),
                rhs_scale=planes[u][:],
                start=True,
                stop=True,
            )

        def sig_product(u, h):
            acc = banks.tile([P, UNIT_ROWS], F32, tag="aux", bufs=AUX_BANKS)
            product(acc, 1, h, u)
            held["sig", u, h] = acc

        def capped(u, h):
            if h == 0:
                soft[u] = enc.tile([P, HALVES, UNIT_ROWS], F32, name="soft", bufs=2)
            nc.vector.tensor_scalar(
                out=soft[u][:, h, :], in0=held["sig", u, h][:],
                scalar1=params[:, h, ROW_BE_SIG : ROW_BE_SIG + 1], scalar2=SOFT_CAP, op0=ALU.add, op1=ALU.min,
            )

        def soft_exp(u):
            nc.scalar.activation(out=soft[u][:], in_=soft[u][:], func=ACT.Exp)

        def half_exp(u, h):
            nc.scalar.activation(out=soft[u][:, h, :], in_=soft[u][:, h, :], func=ACT.Exp)

        def soft_log(u):
            nc.scalar.activation(out=soft[u][:], in_=soft[u][:], func=ACT.Ln, bias=ones_col[:])

        def softplus(u, h):
            if h == 0:
                sp_T[u] = enc.tile([P, HALVES, UNIT_ROWS], F32, name="sp_T", bufs=2)
            nc.vector.scalar_tensor_tensor(
                out=sp_T[u][:, h, :], in0=held["sig", u, h][:], scalar=params[:, h, ROW_BE_SIG : ROW_BE_SIG + 1],
                in1=soft[u][:, h, :], op0=ALU.add, op1=ALU.max,
            )

        def first_softplus():
            for h in range(HALVES):
                nc.scalar.activation(out=soft[0][:, h, :], in_=soft[0][:, h, :], func=ACT.Ln, bias=ones_col[:])
                softplus(0, h)

        def mu_product(u):
            for h in range(HALVES):
                acc = banks.tile([P, UNIT_ROWS], F32, tag="mu", bufs=HALVES)
                product(acc, 0, h, u)
                mu_ps[u, h] = acc

        def store(dram, u, pair, out_rows):
            first_tile = u * UNIT_TILES + 2 * pair
            nc.sync.dma_start(out=dram[:, first_tile : first_tile + 2, :], in_=out_rows[:])

        def mu_rows(u, pair):
            bank = banks.tile([P, 2, XD], F32, tag="aux", bufs=AUX_BANKS)
            for two in range(2):
                cols = slice((2 * pair + two) * P, (2 * pair + two + 1) * P)
                nc.tensor.matmul_mx(
                    out=bank[:, two, :],
                    lhsT=codes[u][:, cols].bitcast(FP8X4),
                    lhsT_scale=planes[u][:, cols],
                    rhs=w_words[:, 0, :].bitcast(FP8X4),
                    rhs_scale=w_planes[:, 0, :],
                    start=True,
                    stop=True,
                )
            held["mu", u, pair] = bank

        def store_mu(u, pair):
            out_rows = enc.tile([P, 2, XD], F32, name="out_rows", bufs=3)
            nc.vector.tensor_tensor(
                out=out_rows[:], in0=held["mu", u, pair][:],
                in1=be_mu_rows[:].unsqueeze(1).to_broadcast([P, 2, XD]), op=ALU.add,
            )
            store(mu_out, u, pair, out_rows)

        def sig_rows(u, pair):
            bank = banks.tile([P, 2, XD], F32, tag="aux", bufs=AUX_BANKS)
            for two in range(2):
                first = (2 * pair + two) * P
                for h in range(HALVES):
                    nc.tensor.transpose(
                        out=bank[:, two, h * P : (h + 1) * P], in_=sp_T[u][:, h, first : first + P], identity=ident[:]
                    )
            held["sp", u, pair] = bank

        def store_sig(u, pair):
            out_rows = enc.tile([P, 2, XD], F32, name="out_rows", bufs=3)
            nc.vector.tensor_scalar(
                out=out_rows[:], in0=held["sp", u, pair][:], scalar1=SIG_FLOOR, scalar2=None, op0=ALU.add
            )
            store(sig_out, u, pair, out_rows)

        log_of = {}
        ratio_of = {}
        sums = const.tile([P, TILES, CLUSTERS], F32)

        def squarer(u, k):
            if u == UNITS - 1:
                return "scalar" if k % 2 == 1 or k == CLUSTERS - 2 else "gpsimd"
            return "vector" if k in vector_squares(u) else "gpsimd"

        def pair_product(u, k):
            swapped = ratios.tile([P, HALVES, UNIT_ROWS], F32, name="swapped", bufs=PAIR_BUFS)
            eng = nc.vector if (u == 0 and k in (11, 12)) else nc.gpsimd
            for h in range(HALVES):
                eng.tensor_scalar(
                    out=swapped[:, h, :], in0=sp_T[u][:, 1 - h, :],
                    scalar1=spread[:, 1 - h, k : k + 1], scalar2=1.0, op0=ALU.add, op1=ALU.mult,
                )
            pair_log = logs.tile([P, UNIT_ROWS], F32, name="pair_log", bufs=PAIR_BUFS)
            eng.tensor_tensor(out=pair_log[:], in0=swapped[:, 0, :], in1=swapped[:, 1, :], op=ALU.mult)
            ratio_of[u, k] = swapped
            log_of[u, k] = pair_log

        def pair_inverse(u, k):
            inverse = ratios.tile([P, UNIT_ROWS], F32, name="inverse", bufs=PAIR_BUFS)
            nc.scalar.activation(out=inverse[:], in_=log_of[u, k][:], func=ACT.Exp, scale=-1.0, bias=half_col[:])
            held["inverse", u, k] = inverse

        def pair_ratio(u, k):
            (nc.vector if (u == 0 and k in (11,)) else nc.gpsimd).tensor_tensor(
                out=ratio_of[u, k][:], in0=ratio_of[u, k][:],
                in1=held["inverse", u, k][:].unsqueeze(1).to_broadcast([P, HALVES, UNIT_ROWS]), op=ALU.mult,
            )

        def log_std(u, k):
            if k in paired(u):
                nc.scalar.activation(out=log_of[u, k][:], in_=log_of[u, k][:], func=ACT.Ln)
                return
            log_t = logs.tile([P, HALVES, UNIT_ROWS], F32, name="log_t")
            for h in range(HALVES):
                nc.scalar.activation(
                    out=log_t[:, h, :], in_=sp_T[u][:, h, :], func=ACT.Ln, bias=spread[:, h, k : k + 1]
                )
            log_of[u, k] = log_t

        def inverse_std(u, k):
            if k in paired(u):
                return
            ratio = ratios.tile([P, HALVES, UNIT_ROWS], F32, name="ratio")
            if squarer(u, k) == "vector":
                nc.scalar.activation(out=ratio[:], in_=log_of[u, k][:], func=ACT.Exp, scale=-2.0, bias=full_col[:])
            else:
                nc.scalar.activation(out=ratio[:], in_=log_of[u, k][:], func=ACT.Exp, scale=-1.0, bias=half_col[:])
            ratio_of[u, k] = ratio

        def scaled_difference(u, k):
            for h in range(HALVES):
                nc.vector.scalar_tensor_tensor(
                    out=ratio_of[u, k][:, h, :], in0=mu_ps[u, h][:], scalar=shift[:, h, k : k + 1],
                    in1=ratio_of[u, k][:, h, :], op0=ALU.subtract, op1=ALU.mult,
                )

        def square(u, k):
            ratio = ratio_of[u, k]
            if squarer(u, k) == "vector":
                scaled_difference(u, k)
            elif squarer(u, k) == "scalar":
                nc.scalar.activation(out=ratio[:], in_=ratio[:], func=ACT.Square)
            else:
                nc.gpsimd.tensor_tensor(out=ratio[:], in0=ratio[:], in1=ratio[:], op=ALU.mult)

        def add_up(u, k):
            bank = banks.tile([P, UNIT_TILES, P], F32, tag="sum", bufs=SUM_BANKS)
            for j in range(UNIT_TILES):
                rows = slice(j * P, (j + 1) * P)
                parts = [ratio_of[u, k][:, h, rows] for h in range(HALVES)]
                if k in paired(u):
                    parts.append(log_of[u, k][:, rows])
                else:
                    parts.extend(log_of[u, k][:, h, rows] for h in range(HALVES))
                for n, part in enumerate(parts):
                    nc.tensor.matmul(
                        out=bank[:, j, :], lhsT=part, rhs=ident[:],
                        is_transpose=True, start=(n == 0), stop=(n == len(parts) - 1),
                    )
            held["sum", u, k] = bank

        def sum_columns(step):
            u, k = divmod(step, CLUSTERS)
            nc.vector.tensor_reduce(
                out=sums[:, u * UNIT_TILES : (u + 1) * UNIT_TILES, k], in_=held["sum", u, k][:],
                axis=AXIS.X, op=ALU.add,
            )

        turn_y(0, 0)
        turn_y(0, 1)
        turn_params()
        group_y(0, 0)
        group_y(0, 1)
        quantise(0)
        derive_params()
        turn_y(1, 0)
        turn_y(1, 1)
        sig_product(0, 0)
        group_y(1, 0, nc.scalar.copy)
        group_y(1, 1, nc.scalar.copy)
        sig_product(0, 1)
        capped(0, 0)
        half_exp(0, 0)
        quantise(1)
        capped(0, 1)
        half_exp(0, 1)
        sig_product(1, 0)
        sig_product(1, 1)
        capped(1, 0)
        half_exp(1, 0)
        capped(1, 1)
        half_exp(1, 1)
        sig_product(0, 0)
        sig_product(0, 1)
        first_softplus()
        for k in paired(0):
            pair_product(0, k)
        mu_product(0)
        be_mu_rows = const.tile([P, XD], F32)
        nc.vector.tensor_copy(out=be_mu_rows[:], in_=be_mu_bf[:])
        logits = const.tile([P, CLUSTERS], F32)
        nc.vector.tensor_copy(out=logits[:], in_=logits_bf[:])

        def behind_the_first_logs():
            turn_y(2, 0)
            turn_y(2, 1)
            mu_rows(0, 0)
            group_y(2, 0)
            group_y(2, 1)
            store_mu(0, 0)
            mu_rows(0, 1)
            mu_rows(1, 0)
            mu_rows(1, 1)
            quantise(2)
            store_mu(0, 1)
            store_mu(1, 0)
            store_mu(1, 1)
            sig_rows(0, 0)
            sig_rows(0, 1)
            sig_product(2, 0)
            store_sig(0, 0)
            store_sig(0, 1)
            sig_product(2, 1)
            capped(2, 0)
            capped(2, 1)
            mu_rows(2, 0)
            mu_rows(2, 1)
            store_mu(2, 0)
            store_mu(2, 1)

        def side_work(u):
            vector = {}
            tensor = {}
            if u + 4 < UNITS:
                vector[0] = [lambda: load_y(u + 4)]
            if 0 < u and u + 2 < UNITS:
                vector.setdefault(0, []).append(lambda: capped(u + 2, 0))
                vector[1] = [lambda: capped(u + 2, 1)]
                tensor[2] = [lambda: mu_rows(u + 2, 0)]
                tensor[3] = [lambda: mu_rows(u + 2, 1)]
                vector[5] = [lambda: store_mu(u + 2, 0)]
                vector[6] = [lambda: store_mu(u + 2, 1)]
            if u + 1 < UNITS:
                tensor[0] = [lambda: sig_product(u + 1, 0)]
                tensor[1] = [lambda: sig_product(u + 1, 1)]
                vector[3] = [lambda: softplus(u + 1, 0)]
                vector[4] = [lambda: softplus(u + 1, 1)]
                vector.setdefault(5, []).extend([lambda k=k: pair_product(u + 1, k) for k in paired(u + 1)])
                tensor[6] = [lambda: sig_rows(u + 1, 0)]
                tensor[7] = [lambda: sig_rows(u + 1, 1)]
                vector[9] = [lambda: store_sig(u + 1, 0)]
                vector[10] = [lambda: store_sig(u + 1, 1)]
            if u + 3 < UNITS:
                tensor[9] = [lambda: turn_y(u + 3, 0)]
                tensor[10] = [lambda: turn_y(u + 3, 1)]
                vector[12] = [lambda: group_y(u + 3, 0)]
                vector[13] = [lambda: group_y(u + 3, 1)]
                vector[14] = [lambda: quantise(u + 3)]
                tensor[14] = [lambda: sig_product(u + 3, 0)]
                tensor[15] = [lambda: sig_product(u + 3, 1)]
            if u + 1 < UNITS:
                tensor.setdefault(14, []).append(lambda: mu_product(u + 1))
            return vector, tensor

        z = const.tile([P, TILES, CLUSTERS], F32)
        z_max = const.tile([P, TILES], F32)
        z_sum = const.tile([P, TILES], F32)

        def shifted_logits(a, b):
            nc.vector.scalar_tensor_tensor(
                out=z[:, a:b, :], in0=sums[:, a:b, :], scalar=-1.0,
                in1=logits[:].unsqueeze(1).to_broadcast([P, b - a, CLUSTERS]), op0=ALU.mult, op1=ALU.add,
            )
            nc.vector.tensor_reduce(out=z_max[:, a:b], in_=z[:, a:b, :], axis=AXIS.X, op=ALU.max)
            nc.vector.tensor_tensor(
                out=z[:, a:b, :], in0=z[:, a:b, :],
                in1=z_max[:, a:b].unsqueeze(2).to_broadcast([P, b - a, CLUSTERS]), op=ALU.subtract,
            )

        def logit_exp(a, b):
            nc.scalar.activation(out=sums[:, a:b, :], in_=z[:, a:b, :], func=ACT.Exp)

        def exp_sum(a, b):
            nc.vector.tensor_reduce(out=z_sum[:, a:b], in_=sums[:, a:b, :], axis=AXIS.X, op=ALU.add)

        def sum_log(a, b):
            nc.scalar.activation(out=z_sum[:, a:b], in_=z_sum[:, a:b], func=ACT.Ln)

        def store_z(a, b):
            nc.vector.tensor_tensor(
                out=z[:, a:b, :], in0=z[:, a:b, :],
                in1=z_sum[:, a:b].unsqueeze(2).to_broadcast([P, b - a, CLUSTERS]), op=ALU.subtract,
            )
            nc.sync.dma_start(out=z_out[:, a:b, :], in_=z[:, a:b, :])

        for u in range(UNITS):
            for k in range(CLUSTERS):
                log_std(u, k)
            if u == UNITS - 1:
                sum_log(0, EARLY_TILES)
            if u + 1 < UNITS:
                soft_log(u + 1)
            if u == 0:
                behind_the_first_logs()
            vector_side, tensor_side = side_work(u)
            for j in range(CLUSTERS):
                for k in range(0 if j == 0 else j + 2, min(j + 3, CLUSTERS)):
                    inverse_std(u, k)
                if j == 0:
                    for k in paired(u):
                        pair_inverse(u, k)
                if j == CLUSTERS - 3 and u + 2 < UNITS:
                    soft_exp(u + 2)
                for k in range(0 if j == 0 else j + 1, min(j + 2, CLUSTERS)):
                    scaled_difference(u, k)
                if u * CLUSTERS + j >= SUM_LAG:
                    sum_columns(u * CLUSTERS + j - SUM_LAG)
                for stage in vector_side.get(j, []):
                    stage()
                if u == UNITS - 2 and j == 4:
                    shifted_logits(0, EARLY_TILES)
                if u == UNITS - 2 and j == 13:
                    logit_exp(0, EARLY_TILES)
                if u == UNITS - 2 and j == 14:
                    exp_sum(0, EARLY_TILES)
                if u == UNITS - 1 and j == 0:
                    store_z(0, EARLY_TILES)
                if j == 1:
                    for k in paired(u):
                        pair_ratio(u, k)
                square(u, j)
                for stage in tensor_side.get(j, []):
                    stage()
                add_up(u, j)
        for step in range(UNITS * CLUSTERS - SUM_LAG, UNITS * CLUSTERS):
            sum_columns(step)

        shifted_logits(EARLY_TILES, TILES)
        logit_exp(EARLY_TILES, TILES)
        exp_sum(EARLY_TILES, TILES)
        sum_log(EARLY_TILES, TILES)
        store_z(EARLY_TILES, TILES)
